import numpy as np
import ml_dtypes


def mxq(x, axis, fmt="e4m3"):
    dtype, down = {"e4m3": (ml_dtypes.float8_e4m3fn, 7), "e5m2": (ml_dtypes.float8_e5m2, 14)}[fmt]
    v = np.moveaxis(np.asarray(x, np.float32).astype(ml_dtypes.bfloat16).astype(np.float64), axis, -1)
    blocks = v.reshape(v.shape[:-1] + (-1, 32))
    amax = np.abs(blocks).max(-1, keepdims=True)
    byte = np.maximum(np.where(amax > 0, np.frexp(amax)[1] - 1 + 127, 0) - down, 1)
    scale = np.exp2(byte - 127.0)
    codes = (blocks / scale).astype(np.float32).astype(dtype).astype(np.float64)
    return np.moveaxis((codes * scale).reshape(v.shape), -1, axis)


WIDE = False


def mx_kscale(k):
    if not WIDE:
        return np.ones(k)
    levels = np.array([10, -10, 5, -5, 0])
    a = np.random.permutation(np.resize(levels, k // 512 * 4)).reshape(k // 512, 4)
    idx = np.arange(k)
    return np.exp2(a[idx // 512, idx % 128 // 32])


BF16 = ml_dtypes.bfloat16


def bf(x):
    return np.asarray(x, np.float32).astype(BF16)


def f64(x):
    return np.asarray(x).astype(np.float64)


B, IN_DIM, HID, ATT = 4096, 128, 512, 384
TOTAL = IN_DIM + HID + ATT


def softplus(v):
    return np.logaddexp(v, 0.0)


def sigmoid(v):
    return 1.0 / (1.0 + np.exp(-v))


def setup_inputs():
    s = np.array(mx_kscale(TOTAL), np.float64)
    s[IN_DIM:IN_DIM + HID] = 1.0
    return {"t": 0.0,
            "h_ltc": bf(np.random.standard_normal((B, HID))),
            "x_t": bf(np.random.standard_normal((B, IN_DIM)) * s[:IN_DIM]),
            "context": bf(np.random.standard_normal((B, ATT)) * s[IN_DIM + HID:]),
            "W_gd": bf(np.random.uniform(-1.0, 1.0, (2 * HID, TOTAL)) * 3.0 / np.sqrt(TOTAL) / s[None, :]),
            "b_gd": bf(np.random.uniform(-0.1, 0.1, (2 * HID,))),
            "W_tau": bf(np.random.uniform(-1.0, 1.0, (HID, HID)) * 2.0 / np.sqrt(HID)),
            "b_tau": bf(np.random.uniform(-0.1, 0.1, (HID,))),
            "gleak": bf(np.random.uniform(0.001, 1.0, (HID,))),
            "cm": bf(np.random.uniform(0.4, 0.6, (HID,)))}


def reference(t, h_ltc, x_t, context, W_gd, b_gd, W_tau, b_tau, gleak, cm):
    h = f64(h_ltc)
    combined = np.concatenate([f64(x_t), h, f64(context)], axis=1)
    g_d = (mxq(combined, 1, "e4m3") @ mxq(f64(W_gd), 1, "e4m3").T) + f64(b_gd)
    gate, dynamics = np.split(g_d, 2, axis=1)
    tau = softplus(h @ f64(W_tau).T + f64(b_tau))
    numerator = sigmoid(gate) * np.tanh(dynamics) - h
    denominator = tau + softplus(f64(cm)) + softplus(f64(gleak))
    return numerator / (denominator + 1e-6)

@@ -1,0 +1,368 @@
+from contextlib import ExitStack
+
+import concourse.mybir as mybir
+from concourse.masks import make_identity
+
+F32 = mybir.dt.float32
+BF16 = mybir.dt.bfloat16
+U32 = mybir.dt.uint32
+U8 = mybir.dt.uint8
+FP8X4 = mybir.dt.float8_e4m3fn_x4
+ACT = mybir.ActivationFunctionType
+ALU = mybir.AluOpType
+
+P = 128
+PACK = 4
+K_PASS = P * PACK
+PAIR = 2
+BATCH, IN_DIM, HID, ATT = 4096, 128, 512, 384
+GROUPS = HID // P
+CHUNK = GROUPS * P
+HALF = CHUNK // 2
+N_CHUNKS = BATCH // CHUNK
+ROUND = 2
+N_ROUNDS = N_CHUNKS // ROUND
+RING = 2 * ROUND
+PASS_H, PASS_XC = 0, 1
+GATE, DYNAMICS = 0, 1
+
+FLOPS = 2 * BATCH * (IN_DIM + HID + ATT) * 2 * HID + 2 * BATCH * HID * HID
+
+
+def tile_ltcattentioncell_kernel(
+    tc, t, h_ltc, x_t, context, W_gd, b_gd, W_tau, b_tau, gleak, cm, out
+):
+    nc = tc.nc
+    with ExitStack() as ctx:
+        ctx.enter_context(tc.manual_schedule())
+        const = ctx.enter_context(tc.tile_pool(name="const", bufs=1))
+        rows_pool = ctx.enter_context(tc.tile_pool(name="rows", bufs=RING))
+        keep = ctx.enter_context(tc.tile_pool(name="keep", bufs=RING))
+        work = ctx.enter_context(tc.tile_pool(name="work", bufs=3))
+        psum = ctx.enter_context(tc.psum_pool(name="psum", bufs=8))
+
+        h_dram = h_ltc.rearrange("(c p t) k -> c p (t k)", p=P, t=GROUPS)
+        x_dram = x_t.rearrange("(c p t) k -> c p t k", p=P, t=GROUPS)
+        ctx_dram = context.rearrange("(c p t) k -> c p t k", p=P, t=GROUPS)
+        out_dram = out.rearrange("(c p t) j -> c p t j", p=P, t=GROUPS)
+
+        h_rows, xc_rows = {}, {}
+        h_words = {}
+        codes, scales = {}, {}
+        denom = {}
+        result = {}
+
+        def load_h(c):
+            h_in = rows_pool.tile([P, GROUPS * K_PASS], BF16)
+            nc.sync.dma_start(out=h_in[:], in_=h_dram[c])
+            h_rows[c] = h_in
+
+        def load_xc(c):
+            xc_in = rows_pool.tile([P, GROUPS * K_PASS], BF16)
+            by_row = xc_in[:].rearrange("p (t k) -> p t k", t=GROUPS)
+            nc.sync.dma_start(out=by_row[:, :, 0:IN_DIM], in_=x_dram[c])
+            nc.sync.dma_start(out=by_row[:, :, IN_DIM:K_PASS], in_=ctx_dram[c])
+            xc_rows[c] = xc_in
+
+        def load_w_gd(half, k_pass):
+            w_in = const.tile([P, GROUPS * K_PASS], BF16, name="w_in_%d_%d" % (half, k_pass))
+            by_row = w_in[:].rearrange("p (q k) -> p q k", q=GROUPS)
+            w_half = W_gd[half * HID : (half + 1) * HID, :].rearrange("(p q) k -> p q k", q=GROUPS)
+            if k_pass == PASS_H:
+                nc.sync.dma_start(out=by_row, in_=w_half[:, :, IN_DIM : IN_DIM + HID])
+            else:
+                nc.sync.dma_start(out=by_row[:, :, 0:IN_DIM], in_=w_half[:, :, 0:IN_DIM])
+                nc.sync.dma_start(out=by_row[:, :, IN_DIM:K_PASS], in_=w_half[:, :, IN_DIM + HID :])
+            return w_in
+
+        ident = const.tile([P, P], F32)
+        make_identity(nc, ident[:])
+        ones = const.tile([P, 1], F32)
+        nc.vector.memset(ones[:], 1.0)
+
+        N_VECTORS = 5
+        ROW_B_GATE, ROW_B_DYN, ROW_B_TAU, ROW_GLEAK = 0, 1, 2, 3
+        vec_rows = const.tile([P, HID], BF16)
+        nc.vector.memset(vec_rows[:], 0.0)
+        nc.scalar.dma_start(out=vec_rows[0:2, :], in_=b_gd.rearrange("(r k) -> r k", r=2))
+        nc.scalar.dma_start(out=vec_rows[2:3, :], in_=b_tau.rearrange("(r k) -> r k", r=1))
+        nc.scalar.dma_start(out=vec_rows[3:4, :], in_=gleak.rearrange("(r k) -> r k", r=1))
+        nc.scalar.dma_start(out=vec_rows[4:5, :], in_=cm.rearrange("(r k) -> r k", r=1))
+
+        wt_in = const.tile([P, GROUPS * HID], BF16)
+        nc.sync.dma_start(out=wt_in[:], in_=W_tau.rearrange("(p q) k -> p (q k)", q=GROUPS))
+        load_h(0)
+        load_h(1)
+        w_in = {}
+        for k_pass in (PASS_H, PASS_XC):
+            for half in (GATE, DYNAMICS):
+                w_in[(half, k_pass)] = load_w_gd(half, k_pass)
+        load_xc(0)
+        load_xc(1)
+        load_h(2)
+        load_h(3)
+        load_xc(2)
+        load_xc(3)
+
+        def word_planes(rows_bf16, n_groups):
+            return rows_bf16.bitcast(F32).rearrange("r (g p u) -> r g u p", g=n_groups, u=PAIR)
+
+        def transpose_rows(rows_bf16):
+            planes = word_planes(rows_bf16, GROUPS)
+            banks = []
+            for b in range(2):
+                bank = psum.tile([P, PAIR * HALF], F32, tag="bank")
+                cells = bank[:].rearrange("p (u g r) -> p u g r", u=PAIR, g=2)
+                for g in range(2):
+                    for u in range(PAIR):
+                        nc.tensor.transpose(cells[:, u, g, :], planes[:, 2 * b + g, u, :], ident[:])
+                banks.append(bank)
+            return banks
+
+        def take_in(jobs):
+            waiting = None
+            for rows_bf16, kept, codes_ap, scales_ap in jobs:
+                banks = transpose_rows(rows_bf16)
+                grouped = work.tile([P, PAIR * CHUNK], F32, align_bytes=64)
+                by_column = grouped[:].rearrange("p (c u) -> p c u", u=PAIR)
+                if kept is not None:
+                    by_plane = kept[:].rearrange("p (u c) -> p u c", u=PAIR)
+                    for b in range(2):
+                        nc.vector.tensor_copy(
+                            out=by_plane[:, :, b * HALF : (b + 1) * HALF],
+                            in_=banks[b][:].rearrange("p (u c) -> p u c", u=PAIR),
+                        )
+                for b in range(2):
+                    nc.vector.tensor_copy(
+                        out=by_column[:, b * HALF : (b + 1) * HALF, :],
+                        in_=banks[b][:].rearrange("p (u c) -> p c u", u=PAIR),
+                    )
+                if waiting is not None:
+                    quantise(*waiting)
+                waiting = (grouped, codes_ap, scales_ap)
+            quantise(*waiting)
+
+        def quantise(grouped, codes_ap, scales_ap):
+            nc.vector.quantize_mx(
+                out=codes_ap.bitcast(FP8X4), scales=scales_ap, in_=grouped[:].bitcast(BF16)
+            )
+
+        def pass_columns(k_pass, width):
+            return slice(k_pass * width, (k_pass + 1) * width)
+
+        def h_jobs(chunks):
+            jobs = []
+            for c in chunks:
+                h_t = keep.tile([P, PAIR * CHUNK], F32)
+                c_codes = keep.tile([P, 2 * CHUNK], U32, align_bytes=64)
+                c_scales = keep.tile([P, 2 * CHUNK], U8, align_bytes=64)
+                h_words[c], codes[c], scales[c] = h_t, c_codes, c_scales
+                cols = pass_columns(PASS_H, CHUNK)
+                jobs.append((h_rows[c][:], h_t, c_codes[:, cols], c_scales[:, cols]))
+            return jobs
+
+        def xc_jobs(chunks):
+            cols = pass_columns(PASS_XC, CHUNK)
+            return [(xc_rows[c][:], None, codes[c][:, cols], scales[c][:, cols]) for c in chunks]
+
+        def chunks_of(r):
+            return list(range(r * ROUND, (r + 1) * ROUND)) if 0 <= r < N_ROUNDS else []
+
+        wt_t = const.tile([P, PACK * HID], BF16)
+        wt_cells = wt_t[:].rearrange("p (u e c) -> p u e c", u=PAIR, e=PAIR)
+        wt_banks = transpose_rows(wt_in[:])
+        for b in range(2):
+            nc.scalar.copy(
+                out=wt_cells[:, :, :, b * HALF : (b + 1) * HALF],
+                in_=wt_banks[b][:].bitcast(BF16).rearrange("p (u c e) -> p u e c", u=PAIR, e=PAIR),
+            )
+
+        def time_constant(c, u):
+            h_bf16 = h_words[c][:].bitcast(BF16).rearrange("p (v c e) -> p v e c", v=PAIR, e=PAIR)
+            for q in (2 * u, 2 * u + 1):
+                z = psum.tile([P, CHUNK], F32, tag="bank")
+                for k_group in range(PACK):
+                    v, e = divmod(k_group, PAIR)
+                    nc.tensor.matmul(
+                        out=z[:],
+                        lhsT=wt_cells[:, v, e, q * P : (q + 1) * P],
+                        rhs=h_bf16[:, v, e, :],
+                        start=(k_group == 0),
+                        stop=(k_group == PACK - 1),
+                    )
+                nc.scalar.activation(
+                    out=denom[c][:, q * CHUNK : (q + 1) * CHUNK],
+                    in_=z[:],
+                    func=ACT.Exp,
+                    bias=vector_column(ROW_B_TAU, q),
+                    scale=1.0,
+                )
+
+        def logarithms(chunks):
+            for c in chunks:
+                nc.scalar.activation(out=denom[c][:], in_=denom[c][:], func=ACT.Ln, bias=ones[:], scale=1.0)
+            for c in chunks:
+                for q in range(GROUPS):
+                    cols = slice(q * CHUNK, (q + 1) * CHUNK)
+                    nc.scalar.activation(
+                        out=denom[c][:, cols], in_=denom[c][:, cols], func=ACT.Ln, bias=leak[:, q : q + 1], scale=1.0
+                    )
+
+        def reciprocal(c, u):
+            nc.scalar.activation(out=group_pair(denom[c], u), in_=group_pair(denom[c], u), func=ACT.Exp, scale=-1.0)
+
+        def gate_times_dynamics(c, u):
+            tanhs = []
+            for half in (GATE, DYNAMICS):
+                tanh_out = work.tile([P, PAIR * CHUNK], F32, tag="tanh_%d" % half)
+                for e in range(PAIR):
+                    q = 2 * u + e
+                    acc = psum.tile([P, CHUNK], F32, tag="bank")
+                    for k_pass in (PASS_H, PASS_XC):
+                        w_cols = slice(
+                            k_pass * 2 * HID + half * HID + q * P, k_pass * 2 * HID + half * HID + (q + 1) * P
+                        )
+                        c_cols = pass_columns(k_pass, CHUNK)
+                        nc.tensor.matmul_mx(
+                            out=acc[:],
+                            lhsT=w_codes[:, w_cols].bitcast(FP8X4),
+                            lhsT_scale=w_scales[:, w_cols],
+                            rhs=codes[c][:, c_cols].bitcast(FP8X4),
+                            rhs_scale=scales[c][:, c_cols],
+                            start=(k_pass == PASS_H),
+                            stop=(k_pass == PASS_XC),
+                        )
+                    nc.scalar.activation(
+                        out=tanh_out[:, e * CHUNK : (e + 1) * CHUNK],
+                        in_=acc[:],
+                        func=ACT.Tanh,
+                        bias=half_b_gate[:, q : q + 1] if half == GATE else vector_column(ROW_B_DYN, q),
+                        scale=0.5 if half == GATE else 1.0,
+                    )
+                tanhs.append(tanh_out)
+            nc.vector.scalar_tensor_tensor(
+                out=tanhs[GATE][:], in0=tanhs[GATE][:], scalar=1.0, in1=tanhs[DYNAMICS][:], op0=ALU.add, op1=ALU.mult
+            )
+            return tanhs[GATE]
+
+        def group_pair(tile_ap, u):
+            return tile_ap[:, u * PAIR * CHUNK : (u + 1) * PAIR * CHUNK]
+
+        def subtract_h(product, c, u):
+            h_bf16 = h_words[c][:].bitcast(BF16).rearrange("p (v c e) -> p v e c", v=PAIR, e=PAIR)
+            nc.vector.scalar_tensor_tensor(
+                out=group_pair(result[c], u).rearrange("p (e c) -> p e c", e=PAIR),
+                in0=product[:].rearrange("p (e c) -> p e c", e=PAIR),
+                scalar=0.5,
+                in1=h_bf16[:, u, :, :],
+                op0=ALU.mult,
+                op1=ALU.subtract,
+            )
+
+        def divide(c, u):
+            nc.vector.tensor_tensor(
+                out=group_pair(result[c], u), in0=group_pair(result[c], u), in1=group_pair(denom[c], u), op=ALU.mult
+            )
+
+        def put_out(c, t_group, scalar_helps):
+            bank = psum.tile([P, HID], F32, tag="bank")
+            for q in range(GROUPS):
+                first = q * CHUNK + t_group * P
+                nc.tensor.transpose(bank[:, q * P : (q + 1) * P], result[c][:, first : first + P], ident[:])
+            rows_out = work.tile([P, HID], F32, bufs=8)
+            copy = nc.scalar.copy if scalar_helps and t_group % 2 == 0 else nc.vector.tensor_copy
+            copy(
+                out=rows_out[:].rearrange("p (j q) -> p j q", q=GROUPS),
+                in_=bank[:].rearrange("p (q j) -> p j q", q=GROUPS),
+            )
+            nc.sync.dma_start(out=out_dram[c][:, t_group, :], in_=rows_out[:])
+
+        def open_denominators(chunks):
+            for c in chunks:
+                d = keep.tile([P, GROUPS * CHUNK], F32)
+                denom[c] = d
+
+        leak_exp = const.tile([P, 2 * GROUPS], F32)
+        leak_softplus = const.tile([P, 2 * GROUPS], F32)
+        leak_sum = const.tile([P, GROUPS], F32)
+        leak = const.tile([P, GROUPS], F32)
+        vectors = const.tile([P, N_VECTORS * GROUPS], F32)
+        vec_cells = vectors[:].rearrange("p (r u e) -> p r u e", u=PAIR, e=PAIR)
+        vec_planes = word_planes(vec_rows[:], 1)
+        vec_bank = psum.tile([P, PAIR * HALF], F32, tag="bank")
+        for u in range(PAIR):
+            nc.tensor.transpose(vec_bank[:, u * P : (u + 1) * P], vec_planes[:, 0, u, :], ident[:])
+        for u in range(PAIR):
+            nc.vector.tensor_copy(
+                out=vec_cells[:, :, u, :],
+                in_=vec_bank[:, u * P : u * P + N_VECTORS].bitcast(BF16).rearrange("p (r e) -> p r e", e=PAIR),
+            )
+
+        def vector_column(row, q):
+            return vectors[:, row * GROUPS + q : row * GROUPS + q + 1]
+
+        half_b_gate = const.tile([P, GROUPS], F32)
+        nc.vector.tensor_scalar_mul(
+            out=half_b_gate[:], in0=vectors[:, ROW_B_GATE * GROUPS : (ROW_B_GATE + 1) * GROUPS], scalar1=0.5
+        )
+
+        take_in(h_jobs(chunks_of(0)))
+        load_h(RING)
+        load_h(RING + 1)
+
+        nc.scalar.activation(out=leak_exp[:], in_=vectors[:, ROW_GLEAK * GROUPS :], func=ACT.Exp)
+        open_denominators(chunks_of(0))
+        for c in chunks_of(0):
+            for u in range(PAIR):
+                time_constant(c, u)
+
+        nc.scalar.activation(out=leak_softplus[:], in_=leak_exp[:], func=ACT.Ln, bias=ones[:], scale=1.0)
+        nc.gpsimd.tensor_tensor(
+            out=leak_sum[:], in0=leak_softplus[:, 0:GROUPS], in1=leak_softplus[:, GROUPS:], op=ALU.add
+        )
+        nc.gpsimd.tensor_scalar(out=leak[:], in0=leak_sum[:], scalar1=1e-6, scalar2=1.0, op0=ALU.add, op1=ALU.mult)
+        logarithms(chunks_of(0))
+
+        w_codes = const.tile([P, 2 * 2 * HID], U32, align_bytes=64)
+        w_scales = const.tile([P, 2 * 2 * HID], U8, align_bytes=64)
+        w_jobs = []
+        for k_pass in (PASS_H, PASS_XC):
+            for half in (GATE, DYNAMICS):
+                cols = slice(k_pass * 2 * HID + half * HID, k_pass * 2 * HID + (half + 1) * HID)
+                w_jobs.append((w_in[(half, k_pass)][:], None, w_codes[:, cols], w_scales[:, cols]))
+        take_in(w_jobs + xc_jobs(chunks_of(0)) + h_jobs(chunks_of(1)))
+        load_xc(RING)
+        load_xc(RING + 1)
+        load_h(RING + 2)
+        load_h(RING + 3)
+
+        for r in range(N_ROUNDS):
+            before, now, ahead = chunks_of(r - 1), chunks_of(r), chunks_of(r + 1)
+            open_denominators(ahead)
+            behind = None
+            for i in range(ROUND):
+                res = keep.tile([P, GROUPS * CHUNK], F32)
+                result[now[i]] = res
+                for u in range(PAIR):
+                    product = gate_times_dynamics(now[i], u)
+                    if behind is not None:
+                        divide(*behind)
+                    subtract_h(product, now[i], u)
+                    behind = (now[i], u)
+                    if ahead:
+                        time_constant(ahead[i], u)
+                    reciprocal(now[i], u)
+                    if before:
+                        for t_group in (2 * u, 2 * u + 1):
+                            put_out(before[i], t_group, scalar_helps=not ahead)
+            divide(*behind)
+            logarithms(ahead)
+            jobs = xc_jobs(ahead) + h_jobs(chunks_of(r + 2))
+            if jobs:
+                take_in(jobs)
+            for c in ahead:
+                if c + RING < N_CHUNKS:
+                    load_xc(c + RING)
+        for c in chunks_of(N_ROUNDS - 1):
+            for t_group in range(GROUPS):
+                put_out(c, t_group, scalar_helps=True)

@@ -125,17 +125,15 @@ def tile_ltcattentioncell_kernel(
                 banks = transpose_rows(rows_bf16)
                 grouped = work.tile([P, PAIR * CHUNK], F32, align_bytes=64)
                 by_column = grouped[:].rearrange("p (c u) -> p c u", u=PAIR)
+                planes = [bank[:].rearrange("p (u c) -> p u c", u=PAIR) for bank in banks]
                 if kept is not None:
                     by_plane = kept[:].rearrange("p (u c) -> p u c", u=PAIR)
                     for b in range(2):
-                        nc.vector.tensor_copy(
-                            out=by_plane[:, :, b * HALF : (b + 1) * HALF],
-                            in_=banks[b][:].rearrange("p (u c) -> p u c", u=PAIR),
-                        )
+                        nc.vector.tensor_copy(out=by_plane[:, :, b * HALF : (b + 1) * HALF], in_=planes[b])
+                    planes = [by_plane[:, :, b * HALF : (b + 1) * HALF] for b in range(2)]
                 for b in range(2):
                     nc.vector.tensor_copy(
-                        out=by_column[:, b * HALF : (b + 1) * HALF, :],
-                        in_=banks[b][:].rearrange("p (u c) -> p c u", u=PAIR),
+                        out=by_column[:, b * HALF : (b + 1) * HALF, :], in_=planes[b].rearrange("p u c -> p c u")
                     )
                 if waiting is not None:
                     quantise(*waiting)
@@ -264,13 +262,13 @@ def tile_ltcattentioncell_kernel(
                 out=group_pair(result[c], u), in0=group_pair(result[c], u), in1=group_pair(denom[c], u), op=ALU.mult
             )
 
-        def put_out(c, t_group, scalar_helps):
+        def put_out(c, t_group, scalar_of_two):
             bank = psum.tile([P, HID], F32, tag="bank")
             for q in range(GROUPS):
                 first = q * CHUNK + t_group * P
                 nc.tensor.transpose(bank[:, q * P : (q + 1) * P], result[c][:, first : first + P], ident[:])
             rows_out = work.tile([P, HID], F32, bufs=8)
-            copy = nc.scalar.copy if scalar_helps and t_group % 2 == 0 else nc.vector.tensor_copy
+            copy = nc.scalar.copy if t_group % 2 < scalar_of_two else nc.vector.tensor_copy
             copy(
                 out=rows_out[:].rearrange("p (j q) -> p j q", q=GROUPS),
                 in_=bank[:].rearrange("p (q j) -> p j q", q=GROUPS),
@@ -344,17 +342,17 @@ def tile_ltcattentioncell_kernel(
                 res = keep.tile([P, GROUPS * CHUNK], F32)
                 result[now[i]] = res
                 for u in range(PAIR):
-                    product = gate_times_dynamics(now[i], u)
                     if behind is not None:
                         divide(*behind)
-                    subtract_h(product, now[i], u)
-                    behind = (now[i], u)
+                    product = gate_times_dynamics(now[i], u)
                     if ahead:
                         time_constant(ahead[i], u)
                     reciprocal(now[i], u)
-                    if before:
+                    if before and ahead:
                         for t_group in (2 * u, 2 * u + 1):
-                            put_out(before[i], t_group, scalar_helps=not ahead)
+                            put_out(before[i], t_group, scalar_of_two=0)
+                    subtract_h(product, now[i], u)
+                    behind = (now[i], u)
             divide(*behind)
             logarithms(ahead)
             jobs = xc_jobs(ahead) + h_jobs(chunks_of(r + 2))
@@ -363,6 +361,7 @@ def tile_ltcattentioncell_kernel(
             for c in ahead:
                 if c + RING < N_CHUNKS:
                     load_xc(c + RING)
-        for c in chunks_of(N_ROUNDS - 1):
-            for t_group in range(GROUPS):
-                put_out(c, t_group, scalar_helps=True)
+            if not chunks_of(r + 2):
+                for c in now:
+                    for t_group in range(GROUPS):
+                        put_out(c, t_group, scalar_of_two=0 if ahead else 2 if c < now[-1] else 1)

@@ -20,9 +20,8 @@ GROUPS = HID // P
 CHUNK = GROUPS * P
 HALF = CHUNK // 2
 N_CHUNKS = BATCH // CHUNK
-ROUND = 2
-N_ROUNDS = N_CHUNKS // ROUND
-RING = 2 * ROUND
+ROUNDS = (2, 3, 3)
+OUT_JOBS_IN_SLOT = 2
 PASS_H, PASS_XC = 0, 1
 GATE, DYNAMICS = 0, 1
 
@@ -36,9 +35,7 @@ def tile_ltcattentioncell_kernel(
     with ExitStack() as ctx:
         ctx.enter_context(tc.manual_schedule())
         const = ctx.enter_context(tc.tile_pool(name="const", bufs=1))
-        rows_pool = ctx.enter_context(tc.tile_pool(name="rows", bufs=RING))
-        keep = ctx.enter_context(tc.tile_pool(name="keep", bufs=RING))
-        work = ctx.enter_context(tc.tile_pool(name="work", bufs=3))
+        pool = ctx.enter_context(tc.tile_pool(name="pool", bufs=6))
         psum = ctx.enter_context(tc.psum_pool(name="psum", bufs=8))
 
         h_dram = h_ltc.rearrange("(c p t) k -> c p (t k)", p=P, t=GROUPS)
@@ -47,36 +44,38 @@ def tile_ltcattentioncell_kernel(
         out_dram = out.rearrange("(c p t) j -> c p t j", p=P, t=GROUPS)
 
         h_rows, xc_rows = {}, {}
-        h_words = {}
+        h_cols = {}
         codes, scales = {}, {}
         denom = {}
-        result = {}
+        product = {}
 
         def load_h(c):
-            h_in = rows_pool.tile([P, GROUPS * K_PASS], BF16)
+            h_in = pool.tile([P, GROUPS * K_PASS], BF16, bufs=8)
             nc.sync.dma_start(out=h_in[:], in_=h_dram[c])
             h_rows[c] = h_in
 
         def load_xc(c):
-            xc_in = rows_pool.tile([P, GROUPS * K_PASS], BF16)
+            xc_in = pool.tile([P, GROUPS * K_PASS], BF16, tag="rows", bufs=5)
             by_row = xc_in[:].rearrange("p (t k) -> p t k", t=GROUPS)
             nc.sync.dma_start(out=by_row[:, :, 0:IN_DIM], in_=x_dram[c])
             nc.sync.dma_start(out=by_row[:, :, IN_DIM:K_PASS], in_=ctx_dram[c])
             xc_rows[c] = xc_in
 
         def load_w_gd(half, k_pass):
-            w_in = const.tile([P, GROUPS * K_PASS], BF16, name="w_in_%d_%d" % (half, k_pass))
-            by_row = w_in[:].rearrange("p (q k) -> p q k", q=GROUPS)
-            w_half = W_gd[half * HID : (half + 1) * HID, :].rearrange("(p q) k -> p q k", q=GROUPS)
+            w_tile = pool.tile([P, GROUPS * K_PASS], BF16, tag="rows", bufs=5)
+            by_row = w_tile[:].rearrange("p (q k) -> p q k", q=GROUPS)
+            w_half = W_gd[half * HID : (half + 1) * HID, :].rearrange("(q p) k -> p q k", q=GROUPS)
             if k_pass == PASS_H:
                 nc.sync.dma_start(out=by_row, in_=w_half[:, :, IN_DIM : IN_DIM + HID])
             else:
                 nc.sync.dma_start(out=by_row[:, :, 0:IN_DIM], in_=w_half[:, :, 0:IN_DIM])
                 nc.sync.dma_start(out=by_row[:, :, IN_DIM:K_PASS], in_=w_half[:, :, IN_DIM + HID :])
-            return w_in
+            return w_tile
 
         ident = const.tile([P, P], F32)
         make_identity(nc, ident[:])
+        ident_bf16 = const.tile([P, P], BF16)
+        nc.vector.tensor_copy(out=ident_bf16[:], in_=ident[:])
         ones = const.tile([P, 1], F32)
         nc.vector.memset(ones[:], 1.0)
 
@@ -89,26 +88,20 @@ def tile_ltcattentioncell_kernel(
         nc.scalar.dma_start(out=vec_rows[3:4, :], in_=gleak.rearrange("(r k) -> r k", r=1))
         nc.scalar.dma_start(out=vec_rows[4:5, :], in_=cm.rearrange("(r k) -> r k", r=1))
 
-        wt_in = const.tile([P, GROUPS * HID], BF16)
-        nc.sync.dma_start(out=wt_in[:], in_=W_tau.rearrange("(p q) k -> p (q k)", q=GROUPS))
+        wt_in = pool.tile([P, GROUPS * HID], BF16, tag="rows", bufs=5)
+        nc.sync.dma_start(
+            out=wt_in[:].rearrange("p (q k) -> p q k", q=GROUPS), in_=W_tau.rearrange("(q p) k -> p q k", q=GROUPS)
+        )
         load_h(0)
         load_h(1)
         w_in = {}
         for k_pass in (PASS_H, PASS_XC):
             for half in (GATE, DYNAMICS):
                 w_in[(half, k_pass)] = load_w_gd(half, k_pass)
-        load_xc(0)
-        load_xc(1)
-        load_h(2)
-        load_h(3)
-        load_xc(2)
-        load_xc(3)
 
-        def word_planes(rows_bf16, n_groups):
-            return rows_bf16.bitcast(F32).rearrange("r (g p u) -> r g u p", g=n_groups, u=PAIR)
-
-        def transpose_rows(rows_bf16):
-            planes = word_planes(rows_bf16, GROUPS)
+        def transpose_rows(rows_bf16, contiguous):
+            order = "r (g u p) -> r g u p" if contiguous else "r (g p u) -> r g u p"
+            planes = rows_bf16.bitcast(F32).rearrange(order, g=GROUPS, u=PAIR)
             banks = []
             for b in range(2):
                 bank = psum.tile([P, PAIR * HALF], F32, tag="bank")
@@ -119,72 +112,106 @@ def tile_ltcattentioncell_kernel(
                 banks.append(bank)
             return banks
 
-        def take_in(jobs):
-            waiting = None
-            for rows_bf16, kept, codes_ap, scales_ap in jobs:
-                banks = transpose_rows(rows_bf16)
-                grouped = work.tile([P, PAIR * CHUNK], F32, align_bytes=64)
-                by_column = grouped[:].rearrange("p (c u) -> p c u", u=PAIR)
-                planes = [bank[:].rearrange("p (u c) -> p u c", u=PAIR) for bank in banks]
-                if kept is not None:
-                    by_plane = kept[:].rearrange("p (u c) -> p u c", u=PAIR)
-                    for b in range(2):
-                        nc.vector.tensor_copy(out=by_plane[:, :, b * HALF : (b + 1) * HALF], in_=planes[b])
-                    planes = [by_plane[:, :, b * HALF : (b + 1) * HALF] for b in range(2)]
-                for b in range(2):
-                    nc.vector.tensor_copy(
-                        out=by_column[:, b * HALF : (b + 1) * HALF, :], in_=planes[b].rearrange("p u c -> p c u")
-                    )
-                if waiting is not None:
-                    quantise(*waiting)
-                waiting = (grouped, codes_ap, scales_ap)
-            quantise(*waiting)
+        def regroup(banks, grouped):
+            by_column = grouped[:].bitcast(F32).rearrange("p (c u) -> p c u", u=PAIR)
+            for b in range(2):
+                nc.vector.tensor_copy(
+                    out=by_column[:, b * HALF : (b + 1) * HALF, :],
+                    in_=banks[b][:].rearrange("p (u c) -> p c u", u=PAIR),
+                )
 
         def quantise(grouped, codes_ap, scales_ap):
-            nc.vector.quantize_mx(
-                out=codes_ap.bitcast(FP8X4), scales=scales_ap, in_=grouped[:].bitcast(BF16)
-            )
+            nc.vector.quantize_mx(out=codes_ap.bitcast(FP8X4), scales=scales_ap, in_=grouped[:])
 
-        def pass_columns(k_pass, width):
-            return slice(k_pass * width, (k_pass + 1) * width)
+        def h_job(c):
+            def bring():
+                cols = pool.tile([P, PACK * CHUNK], BF16, align_bytes=64, bufs=5, tag="h_cols")
+                c_codes = pool.tile([P, CHUNK], U32, align_bytes=64, bufs=6, tag="h_codes")
+                c_scales = pool.tile([P, CHUNK], U8, align_bytes=64, bufs=6, tag="h_scales")
+                h_cols[c], codes[(c, PASS_H)], scales[(c, PASS_H)] = cols, c_codes, c_scales
+                regroup(transpose_rows(h_rows[c][:], True), cols)
 
-        def h_jobs(chunks):
-            jobs = []
-            for c in chunks:
-                h_t = keep.tile([P, PAIR * CHUNK], F32)
-                c_codes = keep.tile([P, 2 * CHUNK], U32, align_bytes=64)
-                c_scales = keep.tile([P, 2 * CHUNK], U8, align_bytes=64)
-                h_words[c], codes[c], scales[c] = h_t, c_codes, c_scales
-                cols = pass_columns(PASS_H, CHUNK)
-                jobs.append((h_rows[c][:], h_t, c_codes[:, cols], c_scales[:, cols]))
-            return jobs
+            def quant():
+                quantise(h_cols[c], codes[(c, PASS_H)][:], scales[(c, PASS_H)][:])
 
-        def xc_jobs(chunks):
-            cols = pass_columns(PASS_XC, CHUNK)
-            return [(xc_rows[c][:], None, codes[c][:, cols], scales[c][:, cols]) for c in chunks]
+            return bring, quant
 
-        def chunks_of(r):
-            return list(range(r * ROUND, (r + 1) * ROUND)) if 0 <= r < N_ROUNDS else []
+        def xc_job(c):
+            state = {}
 
-        wt_t = const.tile([P, PACK * HID], BF16)
-        wt_cells = wt_t[:].rearrange("p (u e c) -> p u e c", u=PAIR, e=PAIR)
-        wt_banks = transpose_rows(wt_in[:])
-        for b in range(2):
-            nc.scalar.copy(
-                out=wt_cells[:, :, :, b * HALF : (b + 1) * HALF],
-                in_=wt_banks[b][:].bitcast(BF16).rearrange("p (u c e) -> p u e c", u=PAIR, e=PAIR),
-            )
+            def bring():
+                cols = pool.tile([P, PACK * CHUNK], BF16, align_bytes=64, bufs=3, tag="grouped")
+                c_codes = pool.tile([P, CHUNK], U32, align_bytes=64, bufs=4, tag="xc_codes")
+                c_scales = pool.tile([P, CHUNK], U8, align_bytes=64, bufs=4, tag="xc_scales")
+                codes[(c, PASS_XC)], scales[(c, PASS_XC)] = c_codes, c_scales
+                state[0] = cols
+                regroup(transpose_rows(xc_rows[c][:], False), cols)
+
+            def quant():
+                quantise(state[0], codes[(c, PASS_XC)][:], scales[(c, PASS_XC)][:])
+
+            return bring, quant
+
+        def w_job(half, k_pass):
+            state = {}
+
+            def bring():
+                cols = pool.tile([P, PACK * CHUNK], BF16, align_bytes=64, bufs=3, tag="grouped")
+                state[0] = cols
+                regroup(transpose_rows(w_in[(half, k_pass)][:], k_pass == PASS_H), cols)
+
+            def quant():
+                cols = slice((2 * k_pass + half) * HID, (2 * k_pass + half + 1) * HID)
+                quantise(state[0], w_codes[:, cols], w_scales[:, cols])
+
+            return bring, quant
+
+        def out_job(c, t_group):
+            state = {}
+
+            def bring():
+                rows = slice(t_group * HID, (t_group + 1) * HID)
+                bank = psum.tile([P, HID], F32, tag="bank")
+                for q in range(GROUPS):
+                    first = q * CHUNK + t_group * P
+                    nc.tensor.transpose(bank[:, q * P : (q + 1) * P], product[c][:, first : first + P], ident[:])
+                numerator = pool.tile([P, HID], F32, tag="numerator", bufs=4)
+                nc.vector.scalar_tensor_tensor(
+                    out=numerator[:], in0=bank[:], scalar=0.5, in1=h_rows[c][:, rows], op0=ALU.mult, op1=ALU.subtract
+                )
+                bank_r = psum.tile([P, HID], F32, tag="bank")
+                for q in range(GROUPS):
+                    first = q * CHUNK + t_group * P
+                    nc.tensor.transpose(bank_r[:, q * P : (q + 1) * P], denom[c][:, first : first + P], ident[:])
+                state[0] = numerator, bank_r
+
+            def finish():
+                numerator, bank_r = state[0]
+                rows_out = pool.tile([P, HID], F32, tag="rows_out", bufs=6)
+                nc.vector.tensor_tensor(out=rows_out[:], in0=bank_r[:], in1=numerator[:], op=ALU.mult)
+                nc.sync.dma_start(out=out_dram[c][:, t_group, :], in_=rows_out[:])
+
+            return bring, finish
+
+        def run(jobs):
+            waiting = None
+            for first, second in jobs:
+                first()
+                if waiting is not None:
+                    waiting()
+                waiting = second
+            if waiting is not None:
+                waiting()
 
         def time_constant(c, u):
-            h_bf16 = h_words[c][:].bitcast(BF16).rearrange("p (v c e) -> p v e c", v=PAIR, e=PAIR)
+            h_k = h_cols[c][:].rearrange("p (c k) -> p k c", k=PACK)
             for q in (2 * u, 2 * u + 1):
                 z = psum.tile([P, CHUNK], F32, tag="bank")
                 for k_group in range(PACK):
-                    v, e = divmod(k_group, PAIR)
                     nc.tensor.matmul(
                         out=z[:],
-                        lhsT=wt_cells[:, v, e, q * P : (q + 1) * P],
-                        rhs=h_bf16[:, v, e, :],
+                        lhsT=wt_cells[:, k_group, q * P : (q + 1) * P],
+                        rhs=h_k[:, k_group, :],
                         start=(k_group == 0),
                         stop=(k_group == PACK - 1),
                     )
@@ -203,98 +230,89 @@ def tile_ltcattentioncell_kernel(
                 for q in range(GROUPS):
                     cols = slice(q * CHUNK, (q + 1) * CHUNK)
                     nc.scalar.activation(
-                        out=denom[c][:, cols], in_=denom[c][:, cols], func=ACT.Ln, bias=leak[:, q : q + 1], scale=1.0
+                        out=denom[c][:, cols],
+                        in_=denom[c][:, cols],
+                        func=ACT.Abs_reciprocal_sqrt,
+                        bias=leak[:, q : q + 1],
+                        scale=1.0,
                     )
 
         def reciprocal(c, u):
-            nc.scalar.activation(out=group_pair(denom[c], u), in_=group_pair(denom[c], u), func=ACT.Exp, scale=-1.0)
+            pair = group_pair(denom[c], u)
+            nc.gpsimd.tensor_tensor(out=pair, in0=pair, in1=pair, op=ALU.mult)
+
+        def group_pair(tile_ap, u):
+            return tile_ap[:, u * PAIR * CHUNK : (u + 1) * PAIR * CHUNK]
 
         def gate_times_dynamics(c, u):
-            tanhs = []
+            dynamics = pool.tile([P, PAIR * CHUNK], F32, tag="dynamics", bufs=3)
+            targets = {GATE: group_pair(product[c], u), DYNAMICS: dynamics[:]}
             for half in (GATE, DYNAMICS):
-                tanh_out = work.tile([P, PAIR * CHUNK], F32, tag="tanh_%d" % half)
                 for e in range(PAIR):
                     q = 2 * u + e
                     acc = psum.tile([P, CHUNK], F32, tag="bank")
                     for k_pass in (PASS_H, PASS_XC):
-                        w_cols = slice(
-                            k_pass * 2 * HID + half * HID + q * P, k_pass * 2 * HID + half * HID + (q + 1) * P
-                        )
-                        c_cols = pass_columns(k_pass, CHUNK)
+                        first = (2 * k_pass + half) * HID + q * P
                         nc.tensor.matmul_mx(
                             out=acc[:],
-                            lhsT=w_codes[:, w_cols].bitcast(FP8X4),
-                            lhsT_scale=w_scales[:, w_cols],
-                            rhs=codes[c][:, c_cols].bitcast(FP8X4),
-                            rhs_scale=scales[c][:, c_cols],
+                            lhsT=w_codes[:, first : first + P].bitcast(FP8X4),
+                            lhsT_scale=w_scales[:, first : first + P],
+                            rhs=codes[(c, k_pass)][:].bitcast(FP8X4),
+                            rhs_scale=scales[(c, k_pass)][:],
                             start=(k_pass == PASS_H),
                             stop=(k_pass == PASS_XC),
                         )
                     nc.scalar.activation(
-                        out=tanh_out[:, e * CHUNK : (e + 1) * CHUNK],
+                        out=targets[half][:, e * CHUNK : (e + 1) * CHUNK],
                         in_=acc[:],
                         func=ACT.Tanh,
                         bias=half_b_gate[:, q : q + 1] if half == GATE else vector_column(ROW_B_DYN, q),
                         scale=0.5 if half == GATE else 1.0,
                     )
-                tanhs.append(tanh_out)
+            return dynamics
+
+        def multiply(c, u, dynamics):
+            pair = group_pair(product[c], u)
             nc.vector.scalar_tensor_tensor(
-                out=tanhs[GATE][:], in0=tanhs[GATE][:], scalar=1.0, in1=tanhs[DYNAMICS][:], op0=ALU.add, op1=ALU.mult
+                out=pair, in0=pair, scalar=1.0, in1=dynamics[:], op0=ALU.add, op1=ALU.mult
             )
-            return tanhs[GATE]
-
-        def group_pair(tile_ap, u):
-            return tile_ap[:, u * PAIR * CHUNK : (u + 1) * PAIR * CHUNK]
-
-        def subtract_h(product, c, u):
-            h_bf16 = h_words[c][:].bitcast(BF16).rearrange("p (v c e) -> p v e c", v=PAIR, e=PAIR)
-            nc.vector.scalar_tensor_tensor(
-                out=group_pair(result[c], u).rearrange("p (e c) -> p e c", e=PAIR),
-                in0=product[:].rearrange("p (e c) -> p e c", e=PAIR),
-                scalar=0.5,
-                in1=h_bf16[:, u, :, :],
-                op0=ALU.mult,
-                op1=ALU.subtract,
-            )
-
-        def divide(c, u):
-            nc.vector.tensor_tensor(
-                out=group_pair(result[c], u), in0=group_pair(result[c], u), in1=group_pair(denom[c], u), op=ALU.mult
-            )
-
-        def put_out(c, t_group, scalar_of_two):
-            bank = psum.tile([P, HID], F32, tag="bank")
-            for q in range(GROUPS):
-                first = q * CHUNK + t_group * P
-                nc.tensor.transpose(bank[:, q * P : (q + 1) * P], result[c][:, first : first + P], ident[:])
-            rows_out = work.tile([P, HID], F32, bufs=8)
-            copy = nc.scalar.copy if t_group % 2 < scalar_of_two else nc.vector.tensor_copy
-            copy(
-                out=rows_out[:].rearrange("p (j q) -> p j q", q=GROUPS),
-                in_=bank[:].rearrange("p (q j) -> p j q", q=GROUPS),
-            )
-            nc.sync.dma_start(out=out_dram[c][:, t_group, :], in_=rows_out[:])
 
         def open_denominators(chunks):
             for c in chunks:
-                d = keep.tile([P, GROUPS * CHUNK], F32)
+                d = pool.tile([P, GROUPS * CHUNK], F32, tag="denom", bufs=6)
                 denom[c] = d
+
+        def chunks_of(r):
+            return list(range(sum(ROUNDS[:r]), sum(ROUNDS[: r + 1]))) if 0 <= r < len(ROUNDS) else []
+
+        wt_t = const.tile([P, PACK * HID], BF16)
+        wt_cells = wt_t[:].rearrange("p (k c) -> p k c", k=PACK)
+        wt_split = wt_t[:].rearrange("p (u e c) -> p u e c", u=PAIR, e=PAIR)
+        wt_banks = transpose_rows(wt_in[:], True)
+        for b in range(2):
+            nc.scalar.copy(
+                out=wt_split[:, :, :, b * HALF : (b + 1) * HALF],
+                in_=wt_banks[b][:].bitcast(BF16).rearrange("p (u c e) -> p u e c", u=PAIR, e=PAIR),
+            )
+
+        first_jobs = [h_job(c) for c in chunks_of(0)]
+        for bring, quant in first_jobs:
+            bring()
 
         leak_exp = const.tile([P, 2 * GROUPS], F32)
         leak_softplus = const.tile([P, 2 * GROUPS], F32)
         leak_sum = const.tile([P, GROUPS], F32)
         leak = const.tile([P, GROUPS], F32)
         vectors = const.tile([P, N_VECTORS * GROUPS], F32)
-        vec_cells = vectors[:].rearrange("p (r u e) -> p r u e", u=PAIR, e=PAIR)
-        vec_planes = word_planes(vec_rows[:], 1)
-        vec_bank = psum.tile([P, PAIR * HALF], F32, tag="bank")
-        for u in range(PAIR):
-            nc.tensor.transpose(vec_bank[:, u * P : (u + 1) * P], vec_planes[:, 0, u, :], ident[:])
-        for u in range(PAIR):
-            nc.vector.tensor_copy(
-                out=vec_cells[:, :, u, :],
-                in_=vec_bank[:, u * P : u * P + N_VECTORS].bitcast(BF16).rearrange("p (r e) -> p r e", e=PAIR),
+        vec_bank = psum.tile([P, GROUPS * P], BF16, tag="bank")
+        for q in range(GROUPS):
+            nc.tensor.transpose(
+                vec_bank[:, q * P : (q + 1) * P], vec_rows[:, q * P : (q + 1) * P], ident_bf16[:]
             )
+        nc.vector.tensor_copy(
+            out=vectors[:].rearrange("p (r q) -> p r q", q=GROUPS),
+            in_=vec_bank[:].rearrange("p (q r) -> p r q", q=GROUPS)[:, 0:N_VECTORS, :],
+        )
 
         def vector_column(row, q):
             return vectors[:, row * GROUPS + q : row * GROUPS + q + 1]
@@ -303,16 +321,18 @@ def tile_ltcattentioncell_kernel(
         nc.vector.tensor_scalar_mul(
             out=half_b_gate[:], in0=vectors[:, ROW_B_GATE * GROUPS : (ROW_B_GATE + 1) * GROUPS], scalar1=0.5
         )
-
-        take_in(h_jobs(chunks_of(0)))
-        load_h(RING)
-        load_h(RING + 1)
+        for c in chunks_of(0):
+            load_xc(c)
+        for c in chunks_of(1):
+            load_h(c)
 
         nc.scalar.activation(out=leak_exp[:], in_=vectors[:, ROW_GLEAK * GROUPS :], func=ACT.Exp)
         open_denominators(chunks_of(0))
         for c in chunks_of(0):
             for u in range(PAIR):
                 time_constant(c, u)
+        for bring, quant in first_jobs:
+            quant()
 
         nc.scalar.activation(out=leak_softplus[:], in_=leak_exp[:], func=ACT.Ln, bias=ones[:], scale=1.0)
         nc.gpsimd.tensor_tensor(
@@ -323,45 +343,47 @@ def tile_ltcattentioncell_kernel(
 
         w_codes = const.tile([P, 2 * 2 * HID], U32, align_bytes=64)
         w_scales = const.tile([P, 2 * 2 * HID], U8, align_bytes=64)
-        w_jobs = []
-        for k_pass in (PASS_H, PASS_XC):
-            for half in (GATE, DYNAMICS):
-                cols = slice(k_pass * 2 * HID + half * HID, k_pass * 2 * HID + (half + 1) * HID)
-                w_jobs.append((w_in[(half, k_pass)][:], None, w_codes[:, cols], w_scales[:, cols]))
-        take_in(w_jobs + xc_jobs(chunks_of(0)) + h_jobs(chunks_of(1)))
-        load_xc(RING)
-        load_xc(RING + 1)
-        load_h(RING + 2)
-        load_h(RING + 3)
+        jobs = [w_job(half, k_pass) for k_pass in (PASS_H, PASS_XC) for half in (GATE, DYNAMICS)]
+        jobs += [xc_job(c) for c in chunks_of(0)] + [h_job(c) for c in chunks_of(1)]
+        run(jobs)
 
-        for r in range(N_ROUNDS):
-            before, now, ahead = chunks_of(r - 1), chunks_of(r), chunks_of(r + 1)
+        pending = []
+
+        def put_out(n):
+            run([pending.pop(0) for _ in range(min(n, len(pending)))])
+
+        quants = []
+        for r in range(len(ROUNDS)):
+            now, ahead = chunks_of(r), chunks_of(r + 1)
             open_denominators(ahead)
-            behind = None
-            for i in range(ROUND):
-                res = keep.tile([P, GROUPS * CHUNK], F32)
-                result[now[i]] = res
-                for u in range(PAIR):
-                    if behind is not None:
-                        divide(*behind)
-                    product = gate_times_dynamics(now[i], u)
-                    if ahead:
-                        time_constant(ahead[i], u)
-                    reciprocal(now[i], u)
-                    if before and ahead:
-                        for t_group in (2 * u, 2 * u + 1):
-                            put_out(before[i], t_group, scalar_of_two=0)
-                    subtract_h(product, now[i], u)
-                    behind = (now[i], u)
-            divide(*behind)
-            logarithms(ahead)
-            jobs = xc_jobs(ahead) + h_jobs(chunks_of(r + 2))
-            if jobs:
-                take_in(jobs)
             for c in ahead:
-                if c + RING < N_CHUNKS:
-                    load_xc(c + RING)
-            if not chunks_of(r + 2):
-                for c in now:
-                    for t_group in range(GROUPS):
-                        put_out(c, t_group, scalar_of_two=0 if ahead else 2 if c < now[-1] else 1)
+                load_xc(c)
+            for c in chunks_of(r + 2):
+                load_h(c)
+            for i in range(max(len(now), len(ahead))):
+                if i < len(now):
+                    prod = pool.tile([P, GROUPS * CHUNK], F32, tag="product", bufs=3)
+                    product[now[i]] = prod
+                for u in range(PAIR):
+                    if i < len(now):
+                        dynamics = gate_times_dynamics(now[i], u)
+                        reciprocal(now[i], u)
+                        multiply(now[i], u, dynamics)
+                    if i < len(ahead):
+                        time_constant(ahead[i], u)
+                    if quants:
+                        quants.pop(0)()
+                    if not ahead:
+                        put_out(OUT_JOBS_IN_SLOT)
+                if i < len(now):
+                    pending += [out_job(now[i], t_group) for t_group in range(GROUPS)]
+            for q in quants:
+                q()
+            quants = []
+            logarithms(ahead)
+            if ahead:
+                run([xc_job(c) for c in ahead])
+                for bring, quant in [h_job(c) for c in chunks_of(r + 2)]:
+                    bring()
+                    quants.append(quant)
+            put_out(len(pending))

@@ -44,7 +44,7 @@ def tile_ltcattentioncell_kernel(
         out_dram = out.rearrange("(c p t) j -> c p t j", p=P, t=GROUPS)
 
         h_rows, xc_rows = {}, {}
-        h_cols = {}
+        h_words = {}
         codes, scales = {}, {}
         denom = {}
         product = {}
@@ -124,15 +124,30 @@ def tile_ltcattentioncell_kernel(
             nc.vector.quantize_mx(out=codes_ap.bitcast(FP8X4), scales=scales_ap, in_=grouped[:])
 
         def h_job(c):
+            state = {}
+
             def bring():
-                cols = pool.tile([P, PACK * CHUNK], BF16, align_bytes=64, bufs=5, tag="h_cols")
+                words = pool.tile([P, PAIR * CHUNK], F32, bufs=5, tag="h_words")
+                cols = pool.tile([P, PACK * CHUNK], BF16, align_bytes=64, bufs=3, tag="grouped")
                 c_codes = pool.tile([P, CHUNK], U32, align_bytes=64, bufs=6, tag="h_codes")
                 c_scales = pool.tile([P, CHUNK], U8, align_bytes=64, bufs=6, tag="h_scales")
-                h_cols[c], codes[(c, PASS_H)], scales[(c, PASS_H)] = cols, c_codes, c_scales
-                regroup(transpose_rows(h_rows[c][:], True), cols)
+                h_words[c], codes[(c, PASS_H)], scales[(c, PASS_H)] = words, c_codes, c_scales
+                state[0] = cols
+                planes = words[:].rearrange("p (u c) -> p u c", u=PAIR)
+                by_column = cols[:].bitcast(F32).rearrange("p (c u) -> p c u", u=PAIR)
+                for b, bank in enumerate(transpose_rows(h_rows[c][:], True)):
+                    columns = slice(b * HALF, (b + 1) * HALF)
+                    nc.vector.tensor_copy(
+                        out=planes[:, :, columns], in_=bank[:].rearrange("p (u c) -> p u c", u=PAIR)
+                    )
+                for b in range(2):
+                    columns = slice(b * HALF, (b + 1) * HALF)
+                    nc.vector.tensor_copy(
+                        out=by_column[:, columns, :], in_=planes[:, :, columns].rearrange("p u c -> p c u")
+                    )
 
             def quant():
-                quantise(h_cols[c], codes[(c, PASS_H)][:], scales[(c, PASS_H)][:])
+                quantise(state[0], codes[(c, PASS_H)][:], scales[(c, PASS_H)][:])
 
             return bring, quant
 
@@ -204,14 +219,14 @@ def tile_ltcattentioncell_kernel(
                 waiting()
 
         def time_constant(c, u):
-            h_k = h_cols[c][:].rearrange("p (c k) -> p k c", k=PACK)
+            h_bf16 = h_words[c][:].bitcast(BF16).rearrange("p (u c e) -> p u e c", u=PAIR, e=PAIR)
             for q in (2 * u, 2 * u + 1):
                 z = psum.tile([P, CHUNK], F32, tag="bank")
                 for k_group in range(PACK):
                     nc.tensor.matmul(
                         out=z[:],
                         lhsT=wt_cells[:, k_group, q * P : (q + 1) * P],
-                        rhs=h_k[:, k_group, :],
+                        rhs=h_bf16[:, k_group // PAIR, k_group % PAIR, :],
                         start=(k_group == 0),
                         stop=(k_group == PACK - 1),
                     )
@@ -295,9 +310,7 @@ def tile_ltcattentioncell_kernel(
                 in_=wt_banks[b][:].bitcast(BF16).rearrange("p (u c e) -> p u e c", u=PAIR, e=PAIR),
             )
 
-        first_jobs = [h_job(c) for c in chunks_of(0)]
-        for bring, quant in first_jobs:
-            bring()
+        run([h_job(c) for c in chunks_of(0)])
 
         leak_exp = const.tile([P, 2 * GROUPS], F32)
         leak_softplus = const.tile([P, 2 * GROUPS], F32)
@@ -331,8 +344,6 @@ def tile_ltcattentioncell_kernel(
         for c in chunks_of(0):
             for u in range(PAIR):
                 time_constant(c, u)
-        for bring, quant in first_jobs:
-            quant()
 
         nc.scalar.activation(out=leak_softplus[:], in_=leak_exp[:], func=ACT.Ln, bias=ones[:], scale=1.0)
         nc.gpsimd.tensor_tensor(
@@ -352,7 +363,6 @@ def tile_ltcattentioncell_kernel(
         def put_out(n):
             run([pending.pop(0) for _ in range(min(n, len(pending)))])
 
-        quants = []
         for r in range(len(ROUNDS)):
             now, ahead = chunks_of(r), chunks_of(r + 1)
             open_denominators(ahead)
@@ -371,19 +381,11 @@ def tile_ltcattentioncell_kernel(
                         multiply(now[i], u, dynamics)
                     if i < len(ahead):
                         time_constant(ahead[i], u)
-                    if quants:
-                        quants.pop(0)()
                     if not ahead:
                         put_out(OUT_JOBS_IN_SLOT)
                 if i < len(now):
                     pending += [out_job(now[i], t_group) for t_group in range(GROUPS)]
-            for q in quants:
-                q()
-            quants = []
             logarithms(ahead)
             if ahead:
-                run([xc_job(c) for c in ahead])
-                for bring, quant in [h_job(c) for c in chunks_of(r + 2)]:
-                    bring()
-                    quants.append(quant)
+                run([xc_job(c) for c in ahead] + [h_job(c) for c in chunks_of(r + 2)])
             put_out(len(pending))

@@ -20,8 +20,19 @@ GROUPS = HID // P
 CHUNK = GROUPS * P
 HALF = CHUNK // 2
 N_CHUNKS = BATCH // CHUNK
-ROUNDS = (2, 3, 3)
-OUT_JOBS_IN_SLOT = 2
+ROUNDS = (3, 3, 2)
+RSQ = "G"
+HW = 5
+PROD = 3
+DEN = 6
+GR = 3
+CODES = 6
+XCC = 4
+ROWS = 6
+OUT_LAST = 2
+H_FIRST = 1
+SPLIT = 1
+RSQ_EARLY = 0
 PASS_H, PASS_XC = 0, 1
 GATE, DYNAMICS = 0, 1
 
@@ -55,14 +66,14 @@ def tile_ltcattentioncell_kernel(
             h_rows[c] = h_in
 
         def load_xc(c):
-            xc_in = pool.tile([P, GROUPS * K_PASS], BF16, tag="rows", bufs=5)
+            xc_in = pool.tile([P, GROUPS * K_PASS], BF16, tag="rows", bufs=ROWS)
             by_row = xc_in[:].rearrange("p (t k) -> p t k", t=GROUPS)
             nc.sync.dma_start(out=by_row[:, :, 0:IN_DIM], in_=x_dram[c])
             nc.sync.dma_start(out=by_row[:, :, IN_DIM:K_PASS], in_=ctx_dram[c])
             xc_rows[c] = xc_in
 
         def load_w_gd(half, k_pass):
-            w_tile = pool.tile([P, GROUPS * K_PASS], BF16, tag="rows", bufs=5)
+            w_tile = pool.tile([P, GROUPS * K_PASS], BF16, tag="rows", bufs=ROWS)
             by_row = w_tile[:].rearrange("p (q k) -> p q k", q=GROUPS)
             w_half = W_gd[half * HID : (half + 1) * HID, :].rearrange("(q p) k -> p q k", q=GROUPS)
             if k_pass == PASS_H:
@@ -72,6 +83,15 @@ def tile_ltcattentioncell_kernel(
                 nc.sync.dma_start(out=by_row[:, :, IN_DIM:K_PASS], in_=w_half[:, :, IN_DIM + HID :])
             return w_tile
 
+        N_VECTORS = 5
+        ROW_B_GATE, ROW_B_DYN, ROW_B_TAU, ROW_GLEAK = 0, 1, 2, 3
+        vec_rows = const.tile([P, HID], BF16)
+        nc.vector.memset(vec_rows[:], 0.0)
+        nc.scalar.dma_start(out=vec_rows[2:3, :], in_=b_tau.rearrange("(r k) -> r k", r=1))
+        nc.scalar.dma_start(out=vec_rows[0:2, :], in_=b_gd.rearrange("(r k) -> r k", r=2))
+        nc.scalar.dma_start(out=vec_rows[3:4, :], in_=gleak.rearrange("(r k) -> r k", r=1))
+        nc.scalar.dma_start(out=vec_rows[4:5, :], in_=cm.rearrange("(r k) -> r k", r=1))
+
         ident = const.tile([P, P], F32)
         make_identity(nc, ident[:])
         ident_bf16 = const.tile([P, P], BF16)
@@ -79,21 +99,12 @@ def tile_ltcattentioncell_kernel(
         ones = const.tile([P, 1], F32)
         nc.vector.memset(ones[:], 1.0)
 
-        N_VECTORS = 5
-        ROW_B_GATE, ROW_B_DYN, ROW_B_TAU, ROW_GLEAK = 0, 1, 2, 3
-        vec_rows = const.tile([P, HID], BF16)
-        nc.vector.memset(vec_rows[:], 0.0)
-        nc.scalar.dma_start(out=vec_rows[0:2, :], in_=b_gd.rearrange("(r k) -> r k", r=2))
-        nc.scalar.dma_start(out=vec_rows[2:3, :], in_=b_tau.rearrange("(r k) -> r k", r=1))
-        nc.scalar.dma_start(out=vec_rows[3:4, :], in_=gleak.rearrange("(r k) -> r k", r=1))
-        nc.scalar.dma_start(out=vec_rows[4:5, :], in_=cm.rearrange("(r k) -> r k", r=1))
-
-        wt_in = pool.tile([P, GROUPS * HID], BF16, tag="rows", bufs=5)
+        wt_in = pool.tile([P, GROUPS * HID], BF16, tag="rows", bufs=ROWS)
         nc.sync.dma_start(
             out=wt_in[:].rearrange("p (q k) -> p q k", q=GROUPS), in_=W_tau.rearrange("(q p) k -> p q k", q=GROUPS)
         )
-        load_h(0)
-        load_h(1)
+        for c in range(max(2, ROUNDS[0])):
+            load_h(c)
         w_in = {}
         for k_pass in (PASS_H, PASS_XC):
             for half in (GATE, DYNAMICS):
@@ -127,10 +138,10 @@ def tile_ltcattentioncell_kernel(
             state = {}
 
             def bring():
-                words = pool.tile([P, PAIR * CHUNK], F32, bufs=5, tag="h_words")
-                cols = pool.tile([P, PACK * CHUNK], BF16, align_bytes=64, bufs=3, tag="grouped")
-                c_codes = pool.tile([P, CHUNK], U32, align_bytes=64, bufs=6, tag="h_codes")
-                c_scales = pool.tile([P, CHUNK], U8, align_bytes=64, bufs=6, tag="h_scales")
+                words = pool.tile([P, PAIR * CHUNK], F32, bufs=HW, tag="h_words")
+                cols = pool.tile([P, PACK * CHUNK], BF16, align_bytes=64, bufs=GR, tag="grouped")
+                c_codes = pool.tile([P, CHUNK], U32, align_bytes=64, bufs=CODES, tag="h_codes")
+                c_scales = pool.tile([P, CHUNK], U8, align_bytes=64, bufs=CODES, tag="h_scales")
                 h_words[c], codes[(c, PASS_H)], scales[(c, PASS_H)] = words, c_codes, c_scales
                 state[0] = cols
                 planes = words[:].rearrange("p (u c) -> p u c", u=PAIR)
@@ -155,9 +166,9 @@ def tile_ltcattentioncell_kernel(
             state = {}
 
             def bring():
-                cols = pool.tile([P, PACK * CHUNK], BF16, align_bytes=64, bufs=3, tag="grouped")
-                c_codes = pool.tile([P, CHUNK], U32, align_bytes=64, bufs=4, tag="xc_codes")
-                c_scales = pool.tile([P, CHUNK], U8, align_bytes=64, bufs=4, tag="xc_scales")
+                cols = pool.tile([P, PACK * CHUNK], BF16, align_bytes=64, bufs=GR, tag="grouped")
+                c_codes = pool.tile([P, CHUNK], U32, align_bytes=64, bufs=XCC, tag="xc_codes")
+                c_scales = pool.tile([P, CHUNK], U8, align_bytes=64, bufs=XCC, tag="xc_scales")
                 codes[(c, PASS_XC)], scales[(c, PASS_XC)] = c_codes, c_scales
                 state[0] = cols
                 regroup(transpose_rows(xc_rows[c][:], False), cols)
@@ -171,7 +182,7 @@ def tile_ltcattentioncell_kernel(
             state = {}
 
             def bring():
-                cols = pool.tile([P, PACK * CHUNK], BF16, align_bytes=64, bufs=3, tag="grouped")
+                cols = pool.tile([P, PACK * CHUNK], BF16, align_bytes=64, bufs=GR, tag="grouped")
                 state[0] = cols
                 regroup(transpose_rows(w_in[(half, k_pass)][:], k_pass == PASS_H), cols)
 
@@ -181,29 +192,33 @@ def tile_ltcattentioncell_kernel(
 
             return bring, quant
 
+        def turn(tile_qc, t_group):
+            bank = psum.tile([P, HID], F32, tag="bank")
+            for q in range(GROUPS):
+                first = q * CHUNK + t_group * P
+                nc.tensor.transpose(bank[:, q * P : (q + 1) * P], tile_qc[:, first : first + P], ident[:])
+            return bank
+
         def out_job(c, t_group):
             state = {}
 
             def bring():
-                rows = slice(t_group * HID, (t_group + 1) * HID)
-                bank = psum.tile([P, HID], F32, tag="bank")
-                for q in range(GROUPS):
-                    first = q * CHUNK + t_group * P
-                    nc.tensor.transpose(bank[:, q * P : (q + 1) * P], product[c][:, first : first + P], ident[:])
+                bank = turn(product[c], t_group)
                 numerator = pool.tile([P, HID], F32, tag="numerator", bufs=4)
                 nc.vector.scalar_tensor_tensor(
-                    out=numerator[:], in0=bank[:], scalar=0.5, in1=h_rows[c][:, rows], op0=ALU.mult, op1=ALU.subtract
+                    out=numerator[:],
+                    in0=bank[:],
+                    scalar=0.5,
+                    in1=h_rows[c][:, t_group * HID : (t_group + 1) * HID],
+                    op0=ALU.mult,
+                    op1=ALU.subtract,
                 )
-                bank_r = psum.tile([P, HID], F32, tag="bank")
-                for q in range(GROUPS):
-                    first = q * CHUNK + t_group * P
-                    nc.tensor.transpose(bank_r[:, q * P : (q + 1) * P], denom[c][:, first : first + P], ident[:])
-                state[0] = numerator, bank_r
+                state[0] = turn(denom[c], t_group), numerator
 
             def finish():
-                numerator, bank_r = state[0]
+                bank, numerator = state[0]
                 rows_out = pool.tile([P, HID], F32, tag="rows_out", bufs=6)
-                nc.vector.tensor_tensor(out=rows_out[:], in0=bank_r[:], in1=numerator[:], op=ALU.mult)
+                nc.vector.tensor_tensor(out=rows_out[:], in0=bank[:], in1=numerator[:], op=ALU.mult)
                 nc.sync.dma_start(out=out_dram[c][:, t_group, :], in_=rows_out[:])
 
             return bring, finish
@@ -254,16 +269,18 @@ def tile_ltcattentioncell_kernel(
 
         def reciprocal(c, u):
             pair = group_pair(denom[c], u)
-            nc.gpsimd.tensor_tensor(out=pair, in0=pair, in1=pair, op=ALU.mult)
+            (nc.vector if RSQ == "V" else nc.gpsimd).tensor_tensor(out=pair, in0=pair, in1=pair, op=ALU.mult)
 
         def group_pair(tile_ap, u):
             return tile_ap[:, u * PAIR * CHUNK : (u + 1) * PAIR * CHUNK]
 
-        def gate_times_dynamics(c, u):
+        def gate_times_dynamics(c, u, by_half=True):
             dynamics = pool.tile([P, PAIR * CHUNK], F32, tag="dynamics", bufs=3)
             targets = {GATE: group_pair(product[c], u), DYNAMICS: dynamics[:]}
-            for half in (GATE, DYNAMICS):
-                for e in range(PAIR):
+            order = [(half, e) for half in (GATE, DYNAMICS) for e in range(PAIR)]
+            if not by_half:
+                order = [(half, e) for e in range(PAIR) for half in (GATE, DYNAMICS)]
+            for half, e in order:
                     q = 2 * u + e
                     acc = psum.tile([P, CHUNK], F32, tag="bank")
                     for k_pass in (PASS_H, PASS_XC):
@@ -284,6 +301,11 @@ def tile_ltcattentioncell_kernel(
                         bias=half_b_gate[:, q : q + 1] if half == GATE else vector_column(ROW_B_DYN, q),
                         scale=0.5 if half == GATE else 1.0,
                     )
+                    if not by_half and half == DYNAMICS:
+                        cell = product[c][:, q * CHUNK : (q + 1) * CHUNK]
+                        nc.vector.scalar_tensor_tensor(
+                            out=cell, in0=cell, scalar=1.0, in1=dynamics[:, e * CHUNK : (e + 1) * CHUNK], op0=ALU.add, op1=ALU.mult
+                        )
             return dynamics
 
         def multiply(c, u, dynamics):
@@ -292,36 +314,29 @@ def tile_ltcattentioncell_kernel(
                 out=pair, in0=pair, scalar=1.0, in1=dynamics[:], op0=ALU.add, op1=ALU.mult
             )
 
-        def open_denominators(chunks):
-            for c in chunks:
-                d = pool.tile([P, GROUPS * CHUNK], F32, tag="denom", bufs=6)
-                denom[c] = d
-
         def chunks_of(r):
             return list(range(sum(ROUNDS[:r]), sum(ROUNDS[: r + 1]))) if 0 <= r < len(ROUNDS) else []
-
-        wt_t = const.tile([P, PACK * HID], BF16)
-        wt_cells = wt_t[:].rearrange("p (k c) -> p k c", k=PACK)
-        wt_split = wt_t[:].rearrange("p (u e c) -> p u e c", u=PAIR, e=PAIR)
-        wt_banks = transpose_rows(wt_in[:], True)
-        for b in range(2):
-            nc.scalar.copy(
-                out=wt_split[:, :, :, b * HALF : (b + 1) * HALF],
-                in_=wt_banks[b][:].bitcast(BF16).rearrange("p (u c e) -> p u e c", u=PAIR, e=PAIR),
-            )
-
-        run([h_job(c) for c in chunks_of(0)])
 
         leak_exp = const.tile([P, 2 * GROUPS], F32)
         leak_softplus = const.tile([P, 2 * GROUPS], F32)
         leak_sum = const.tile([P, GROUPS], F32)
         leak = const.tile([P, GROUPS], F32)
+        wt_t = const.tile([P, PACK * HID], BF16)
+        wt_cells = wt_t[:].rearrange("p (k c) -> p k c", k=PACK)
+        wt_split = wt_t[:].rearrange("p (u e c) -> p u e c", u=PAIR, e=PAIR)
+        wt_banks = transpose_rows(wt_in[:], True)
+        for b in range(2):
+            (nc.vector.tensor_copy if b else nc.scalar.copy)(
+                out=wt_split[:, :, :, b * HALF : (b + 1) * HALF],
+                in_=wt_banks[b][:].bitcast(BF16).rearrange("p (u c e) -> p u e c", u=PAIR, e=PAIR),
+            )
+
+        first_h = [h_job(c) for c in chunks_of(0)]
+        first_h[0][0]()
         vectors = const.tile([P, N_VECTORS * GROUPS], F32)
         vec_bank = psum.tile([P, GROUPS * P], BF16, tag="bank")
         for q in range(GROUPS):
-            nc.tensor.transpose(
-                vec_bank[:, q * P : (q + 1) * P], vec_rows[:, q * P : (q + 1) * P], ident_bf16[:]
-            )
+            nc.tensor.transpose(vec_bank[:, q * P : (q + 1) * P], vec_rows[:, q * P : (q + 1) * P], ident_bf16[:])
         nc.vector.tensor_copy(
             out=vectors[:].rearrange("p (r q) -> p r q", q=GROUPS),
             in_=vec_bank[:].rearrange("p (q r) -> p r q", q=GROUPS)[:, 0:N_VECTORS, :],
@@ -334,28 +349,36 @@ def tile_ltcattentioncell_kernel(
         nc.vector.tensor_scalar_mul(
             out=half_b_gate[:], in0=vectors[:, ROW_B_GATE * GROUPS : (ROW_B_GATE + 1) * GROUPS], scalar1=0.5
         )
+        for n, (bring, quant) in enumerate(first_h):
+            if n:
+                bring()
+            quant()
+
         for c in chunks_of(0):
             load_xc(c)
         for c in chunks_of(1):
-            load_h(c)
+            if c not in h_rows:
+                load_h(c)
 
+        def time_constants(chunks):
+            for c in chunks:
+                d = pool.tile([P, GROUPS * CHUNK], F32, tag="denom", bufs=DEN)
+                denom[c] = d
+                for u in range(PAIR):
+                    time_constant(c, u)
+
+        time_constants(chunks_of(0))
         nc.scalar.activation(out=leak_exp[:], in_=vectors[:, ROW_GLEAK * GROUPS :], func=ACT.Exp)
-        open_denominators(chunks_of(0))
-        for c in chunks_of(0):
-            for u in range(PAIR):
-                time_constant(c, u)
-
         nc.scalar.activation(out=leak_softplus[:], in_=leak_exp[:], func=ACT.Ln, bias=ones[:], scale=1.0)
         nc.gpsimd.tensor_tensor(
             out=leak_sum[:], in0=leak_softplus[:, 0:GROUPS], in1=leak_softplus[:, GROUPS:], op=ALU.add
         )
         nc.gpsimd.tensor_scalar(out=leak[:], in0=leak_sum[:], scalar1=1e-6, scalar2=1.0, op0=ALU.add, op1=ALU.mult)
-        logarithms(chunks_of(0))
 
         w_codes = const.tile([P, 2 * 2 * HID], U32, align_bytes=64)
         w_scales = const.tile([P, 2 * 2 * HID], U8, align_bytes=64)
         jobs = [w_job(half, k_pass) for k_pass in (PASS_H, PASS_XC) for half in (GATE, DYNAMICS)]
-        jobs += [xc_job(c) for c in chunks_of(0)] + [h_job(c) for c in chunks_of(1)]
+        jobs += [h_job(c) for c in chunks_of(1)] + [xc_job(c) for c in chunks_of(0)]
         run(jobs)
 
         pending = []
@@ -365,27 +388,40 @@ def tile_ltcattentioncell_kernel(
 
         for r in range(len(ROUNDS)):
             now, ahead = chunks_of(r), chunks_of(r + 1)
-            open_denominators(ahead)
+            logarithms(now)
+            put_out(len(pending))
+            for c in now:
+                for u in range(PAIR):
+                    reciprocal(c, u)
             for c in ahead:
                 load_xc(c)
             for c in chunks_of(r + 2):
                 load_h(c)
-            for i in range(max(len(now), len(ahead))):
-                if i < len(now):
-                    prod = pool.tile([P, GROUPS * CHUNK], F32, tag="product", bufs=3)
-                    product[now[i]] = prod
+            time_constants(ahead)
+            h_jobs, xc_jobs = [h_job(c) for c in chunks_of(r + 2)], [xc_job(c) for c in ahead]
+            jobs = h_jobs + xc_jobs if H_FIRST else xc_jobs + h_jobs
+            waiting = None
+            for c in now:
+                prod = pool.tile([P, GROUPS * CHUNK], F32, tag="product", bufs=PROD)
+                product[c] = prod
                 for u in range(PAIR):
-                    if i < len(now):
-                        dynamics = gate_times_dynamics(now[i], u)
-                        reciprocal(now[i], u)
-                        multiply(now[i], u, dynamics)
-                    if i < len(ahead):
-                        time_constant(ahead[i], u)
+                    last = SPLIT and not ahead and c == now[-1] and u == 1
+                    dynamics = gate_times_dynamics(c, u, by_half=not last)
+                    if jobs:
+                        bring, quant = jobs.pop(0)
+                        bring()
+                        if waiting is not None:
+                            waiting()
+                        waiting = quant
+                    if not last:
+                        multiply(c, u, dynamics)
                     if not ahead:
-                        put_out(OUT_JOBS_IN_SLOT)
-                if i < len(now):
-                    pending += [out_job(now[i], t_group) for t_group in range(GROUPS)]
-            logarithms(ahead)
-            if ahead:
-                run([xc_job(c) for c in ahead] + [h_job(c) for c in chunks_of(r + 2)])
-            put_out(len(pending))
+                        put_out(OUT_LAST)
+                pending += [out_job(c, t_group) for t_group in range(GROUPS)]
+            for bring, quant in jobs:
+                bring()
+                waiting()
+                waiting = quant
+            if waiting is not None:
+                waiting()
+        put_out(len(pending))

@@ -32,7 +32,9 @@ ROWS = 6
 OUT_LAST = 2
 H_FIRST = 1
 SPLIT = 1
-RSQ_EARLY = 0
+GROUP_JOBS = 2
+LEFT = 1
+FIRST_SLOT = 1
 PASS_H, PASS_XC = 0, 1
 GATE, DYNAMICS = 0, 1
 
@@ -381,7 +383,7 @@ def tile_ltcattentioncell_kernel(
         jobs += [h_job(c) for c in chunks_of(1)] + [xc_job(c) for c in chunks_of(0)]
         run(jobs)
 
-        pending = []
+        pending, left = [], []
 
         def put_out(n):
             run([pending.pop(0) for _ in range(min(n, len(pending)))])
@@ -389,30 +391,34 @@ def tile_ltcattentioncell_kernel(
         for r in range(len(ROUNDS)):
             now, ahead = chunks_of(r), chunks_of(r + 1)
             logarithms(now)
-            put_out(len(pending))
+            for c in chunks_of(r + 2):
+                load_h(c)
+            for c in ahead:
+                load_xc(c)
+            run([pending.pop(0) for i in range(len(pending))] + left)
             for c in now:
                 for u in range(PAIR):
                     reciprocal(c, u)
-            for c in ahead:
-                load_xc(c)
-            for c in chunks_of(r + 2):
-                load_h(c)
             time_constants(ahead)
             h_jobs, xc_jobs = [h_job(c) for c in chunks_of(r + 2)], [xc_job(c) for c in ahead]
+            n_left = min(LEFT, len(xc_jobs))
+            xc_jobs, left = xc_jobs[: len(xc_jobs) - n_left], xc_jobs[len(xc_jobs) - n_left :]
             jobs = h_jobs + xc_jobs if H_FIRST else xc_jobs + h_jobs
             waiting = None
+            slot = 0
             for c in now:
                 prod = pool.tile([P, GROUPS * CHUNK], F32, tag="product", bufs=PROD)
                 product[c] = prod
                 for u in range(PAIR):
                     last = SPLIT and not ahead and c == now[-1] and u == 1
                     dynamics = gate_times_dynamics(c, u, by_half=not last)
-                    if jobs:
-                        bring, quant = jobs.pop(0)
-                        bring()
-                        if waiting is not None:
-                            waiting()
-                        waiting = quant
+                    if slot >= FIRST_SLOT and (slot - FIRST_SLOT) % GROUP_JOBS == 0:
+                        for bring, quant in [jobs.pop(0) for i in range(min(GROUP_JOBS, len(jobs)))]:
+                            bring()
+                            if waiting is not None:
+                                waiting()
+                            waiting = quant
+                    slot += 1
                     if not last:
                         multiply(c, u, dynamics)
                     if not ahead:

@@ -46,7 +46,16 @@ def tile_ltcattentioncell_kernel(
 ):
     nc = tc.nc
     with ExitStack() as ctx:
-        ctx.enter_context(tc.manual_schedule())
+        ctx.enter_context(
+            tc.manual_schedule(
+                engines={
+                    mybir.EngineType.Activation,
+                    mybir.EngineType.PE,
+                    mybir.EngineType.SP,
+                    mybir.EngineType.Pool,
+                }
+            )
+        )
         const = ctx.enter_context(tc.tile_pool(name="const", bufs=1))
         pool = ctx.enter_context(tc.tile_pool(name="pool", bufs=6))
         psum = ctx.enter_context(tc.psum_pool(name="psum", bufs=8))

@@ -50,7 +50,6 @@ def tile_ltcattentioncell_kernel(
             tc.manual_schedule(
                 engines={
                     mybir.EngineType.Activation,
-                    mybir.EngineType.PE,
                     mybir.EngineType.SP,
                     mybir.EngineType.Pool,
                 }

@@ -149,9 +149,9 @@ def tile_ltcattentioncell_kernel(
 
             def bring():
                 words = pool.tile([P, PAIR * CHUNK], F32, bufs=HW, tag="h_words")
-                cols = pool.tile([P, PACK * CHUNK], BF16, align_bytes=64, bufs=GR, tag="grouped")
-                c_codes = pool.tile([P, CHUNK], U32, align_bytes=64, bufs=CODES, tag="h_codes")
-                c_scales = pool.tile([P, CHUNK], U8, align_bytes=64, bufs=CODES, tag="h_scales")
+                cols = pool.tile([P, PACK * CHUNK], BF16, align_bytes=256, bufs=GR, tag="grouped")
+                c_codes = pool.tile([P, CHUNK], U32, align_bytes=256, bufs=CODES, tag="h_codes")
+                c_scales = pool.tile([P, CHUNK], U8, align_bytes=256, bufs=CODES, tag="h_scales")
                 h_words[c], codes[(c, PASS_H)], scales[(c, PASS_H)] = words, c_codes, c_scales
                 state[0] = cols
                 planes = words[:].rearrange("p (u c) -> p u c", u=PAIR)
@@ -176,9 +176,9 @@ def tile_ltcattentioncell_kernel(
             state = {}
 
             def bring():
-                cols = pool.tile([P, PACK * CHUNK], BF16, align_bytes=64, bufs=GR, tag="grouped")
-                c_codes = pool.tile([P, CHUNK], U32, align_bytes=64, bufs=XCC, tag="xc_codes")
-                c_scales = pool.tile([P, CHUNK], U8, align_bytes=64, bufs=XCC, tag="xc_scales")
+                cols = pool.tile([P, PACK * CHUNK], BF16, align_bytes=256, bufs=GR, tag="grouped")
+                c_codes = pool.tile([P, CHUNK], U32, align_bytes=256, bufs=XCC, tag="xc_codes")
+                c_scales = pool.tile([P, CHUNK], U8, align_bytes=256, bufs=XCC, tag="xc_scales")
                 codes[(c, PASS_XC)], scales[(c, PASS_XC)] = c_codes, c_scales
                 state[0] = cols
                 regroup(transpose_rows(xc_rows[c][:], False), cols)
@@ -192,7 +192,7 @@ def tile_ltcattentioncell_kernel(
             state = {}
 
             def bring():
-                cols = pool.tile([P, PACK * CHUNK], BF16, align_bytes=64, bufs=GR, tag="grouped")
+                cols = pool.tile([P, PACK * CHUNK], BF16, align_bytes=256, bufs=GR, tag="grouped")
                 state[0] = cols
                 regroup(transpose_rows(w_in[(half, k_pass)][:], k_pass == PASS_H), cols)
 
@@ -385,8 +385,8 @@ def tile_ltcattentioncell_kernel(
         )
         nc.gpsimd.tensor_scalar(out=leak[:], in0=leak_sum[:], scalar1=1e-6, scalar2=1.0, op0=ALU.add, op1=ALU.mult)
 
-        w_codes = const.tile([P, 2 * 2 * HID], U32, align_bytes=64)
-        w_scales = const.tile([P, 2 * 2 * HID], U8, align_bytes=64)
+        w_codes = const.tile([P, 2 * 2 * HID], U32, align_bytes=256)
+        w_scales = const.tile([P, 2 * 2 * HID], U8, align_bytes=256)
         jobs = [w_job(half, k_pass) for k_pass in (PASS_H, PASS_XC) for half in (GATE, DYNAMICS)]
         jobs += [h_job(c) for c in chunks_of(1)] + [xc_job(c) for c in chunks_of(0)]
         run(jobs)

from contextlib import ExitStack

import concourse.mybir as mybir
from concourse.masks import make_identity

F32 = mybir.dt.float32
BF16 = mybir.dt.bfloat16
U32 = mybir.dt.uint32
U8 = mybir.dt.uint8
FP8X4 = mybir.dt.float8_e4m3fn_x4
ACT = mybir.ActivationFunctionType
ALU = mybir.AluOpType

P = 128
PACK = 4
K_PASS = P * PACK
PAIR = 2
BATCH, IN_DIM, HID, ATT = 4096, 128, 512, 384
GROUPS = HID // P
CHUNK = GROUPS * P
HALF = CHUNK // 2
N_CHUNKS = BATCH // CHUNK
ROUNDS = (3, 3, 2)
RSQ = "G"
HW = 5
PROD = 3
DEN = 6
GR = 3
CODES = 6
XCC = 4
ROWS = 6
OUT_LAST = 2
H_FIRST = 1
SPLIT = 1
GROUP_JOBS = 2
LEFT = 1
FIRST_SLOT = 1
PASS_H, PASS_XC = 0, 1
GATE, DYNAMICS = 0, 1

FLOPS = 2 * BATCH * (IN_DIM + HID + ATT) * 2 * HID + 2 * BATCH * HID * HID


def tile_ltcattentioncell_kernel(
    tc, t, h_ltc, x_t, context, W_gd, b_gd, W_tau, b_tau, gleak, cm, out
):
    nc = tc.nc
    with ExitStack() as ctx:
        ctx.enter_context(
            tc.manual_schedule(
                engines={
                    mybir.EngineType.Activation,
                    mybir.EngineType.SP,
                    mybir.EngineType.Pool,
                }
            )
        )
        const = ctx.enter_context(tc.tile_pool(name="const", bufs=1))
        pool = ctx.enter_context(tc.tile_pool(name="pool", bufs=6))
        psum = ctx.enter_context(tc.psum_pool(name="psum", bufs=8))

        h_dram = h_ltc.rearrange("(c p t) k -> c p (t k)", p=P, t=GROUPS)
        x_dram = x_t.rearrange("(c p t) k -> c p t k", p=P, t=GROUPS)
        ctx_dram = context.rearrange("(c p t) k -> c p t k", p=P, t=GROUPS)
        out_dram = out.rearrange("(c p t) j -> c p t j", p=P, t=GROUPS)

        h_rows, xc_rows = {}, {}
        h_words = {}
        codes, scales = {}, {}
        denom = {}
        product = {}

        def load_h(c):
            h_in = pool.tile([P, GROUPS * K_PASS], BF16, bufs=8)
            nc.sync.dma_start(out=h_in[:], in_=h_dram[c])
            h_rows[c] = h_in

        def load_xc(c):
            xc_in = pool.tile([P, GROUPS * K_PASS], BF16, tag="rows", bufs=ROWS)
            by_row = xc_in[:].rearrange("p (t k) -> p t k", t=GROUPS)
            nc.sync.dma_start(out=by_row[:, :, 0:IN_DIM], in_=x_dram[c])
            nc.sync.dma_start(out=by_row[:, :, IN_DIM:K_PASS], in_=ctx_dram[c])
            xc_rows[c] = xc_in

        def load_w_gd(half, k_pass):
            w_tile = pool.tile([P, GROUPS * K_PASS], BF16, tag="rows", bufs=ROWS)
            by_row = w_tile[:].rearrange("p (q k) -> p q k", q=GROUPS)
            w_half = W_gd[half * HID : (half + 1) * HID, :].rearrange("(q p) k -> p q k", q=GROUPS)
            if k_pass == PASS_H:
                nc.sync.dma_start(out=by_row, in_=w_half[:, :, IN_DIM : IN_DIM + HID])
            else:
                nc.sync.dma_start(out=by_row[:, :, 0:IN_DIM], in_=w_half[:, :, 0:IN_DIM])
                nc.sync.dma_start(out=by_row[:, :, IN_DIM:K_PASS], in_=w_half[:, :, IN_DIM + HID :])
            return w_tile

        N_VECTORS = 5
        ROW_B_GATE, ROW_B_DYN, ROW_B_TAU, ROW_GLEAK = 0, 1, 2, 3
        vec_rows = const.tile([P, HID], BF16)
        nc.vector.memset(vec_rows[:], 0.0)
        nc.scalar.dma_start(out=vec_rows[2:3, :], in_=b_tau.rearrange("(r k) -> r k", r=1))
        nc.scalar.dma_start(out=vec_rows[0:2, :], in_=b_gd.rearrange("(r k) -> r k", r=2))
        nc.scalar.dma_start(out=vec_rows[3:4, :], in_=gleak.rearrange("(r k) -> r k", r=1))
        nc.scalar.dma_start(out=vec_rows[4:5, :], in_=cm.rearrange("(r k) -> r k", r=1))

        ident = const.tile([P, P], F32)
        make_identity(nc, ident[:])
        ident_bf16 = const.tile([P, P], BF16)
        nc.vector.tensor_copy(out=ident_bf16[:], in_=ident[:])
        ones = const.tile([P, 1], F32)
        nc.vector.memset(ones[:], 1.0)

        wt_in = pool.tile([P, GROUPS * HID], BF16, tag="rows", bufs=ROWS)
        nc.sync.dma_start(
            out=wt_in[:].rearrange("p (q k) -> p q k", q=GROUPS), in_=W_tau.rearrange("(q p) k -> p q k", q=GROUPS)
        )
        for c in range(max(2, ROUNDS[0])):
            load_h(c)
        w_in = {}
        for k_pass in (PASS_H, PASS_XC):
            for half in (GATE, DYNAMICS):
                w_in[(half, k_pass)] = load_w_gd(half, k_pass)

        def transpose_rows(rows_bf16, contiguous):
            order = "r (g u p) -> r g u p" if contiguous else "r (g p u) -> r g u p"
            planes = rows_bf16.bitcast(F32).rearrange(order, g=GROUPS, u=PAIR)
            banks = []
            for b in range(2):
                bank = psum.tile([P, PAIR * HALF], F32, tag="bank")
                cells = bank[:].rearrange("p (u g r) -> p u g r", u=PAIR, g=2)
                for g in range(2):
                    for u in range(PAIR):
                        nc.tensor.transpose(cells[:, u, g, :], planes[:, 2 * b + g, u, :], ident[:])
                banks.append(bank)
            return banks

        def regroup(banks, grouped):
            by_column = grouped[:].bitcast(F32).rearrange("p (c u) -> p c u", u=PAIR)
            for b in range(2):
                nc.vector.tensor_copy(
                    out=by_column[:, b * HALF : (b + 1) * HALF, :],
                    in_=banks[b][:].rearrange("p (u c) -> p c u", u=PAIR),
                )

        def quantise(grouped, codes_ap, scales_ap):
            nc.vector.quantize_mx(out=codes_ap.bitcast(FP8X4), scales=scales_ap, in_=grouped[:])

        def h_job(c):
            state = {}

            def bring():
                words = pool.tile([P, PAIR * CHUNK], F32, bufs=HW, tag="h_words")
                cols = pool.tile([P, PACK * CHUNK], BF16, align_bytes=256, bufs=GR, tag="grouped")
                c_codes = pool.tile([P, CHUNK], U32, align_bytes=256, bufs=CODES, tag="h_codes")
                c_scales = pool.tile([P, CHUNK], U8, align_bytes=256, bufs=CODES, tag="h_scales")
                h_words[c], codes[(c, PASS_H)], scales[(c, PASS_H)] = words, c_codes, c_scales
                state[0] = cols
                planes = words[:].rearrange("p (u c) -> p u c", u=PAIR)
                by_column = cols[:].bitcast(F32).rearrange("p (c u) -> p c u", u=PAIR)
                for b, bank in enumerate(transpose_rows(h_rows[c][:], True)):
                    columns = slice(b * HALF, (b + 1) * HALF)
                    nc.vector.tensor_copy(
                        out=planes[:, :, columns], in_=bank[:].rearrange("p (u c) -> p u c", u=PAIR)
                    )
                for b in range(2):
                    columns = slice(b * HALF, (b + 1) * HALF)
                    nc.vector.tensor_copy(
                        out=by_column[:, columns, :], in_=planes[:, :, columns].rearrange("p u c -> p c u")
                    )

            def quant():
                quantise(state[0], codes[(c, PASS_H)][:], scales[(c, PASS_H)][:])

            return bring, quant

        def xc_job(c):
            state = {}

            def bring():
                cols = pool.tile([P, PACK * CHUNK], BF16, align_bytes=256, bufs=GR, tag="grouped")
                c_codes = pool.tile([P, CHUNK], U32, align_bytes=256, bufs=XCC, tag="xc_codes")
                c_scales = pool.tile([P, CHUNK], U8, align_bytes=256, bufs=XCC, tag="xc_scales")
                codes[(c, PASS_XC)], scales[(c, PASS_XC)] = c_codes, c_scales
                state[0] = cols
                regroup(transpose_rows(xc_rows[c][:], False), cols)

            def quant():
                quantise(state[0], codes[(c, PASS_XC)][:], scales[(c, PASS_XC)][:])

            return bring, quant

        def w_job(half, k_pass):
            state = {}

            def bring():
                cols = pool.tile([P, PACK * CHUNK], BF16, align_bytes=256, bufs=GR, tag="grouped")
                state[0] = cols
                regroup(transpose_rows(w_in[(half, k_pass)][:], k_pass == PASS_H), cols)

            def quant():
                cols = slice((2 * k_pass + half) * HID, (2 * k_pass + half + 1) * HID)
                quantise(state[0], w_codes[:, cols], w_scales[:, cols])

            return bring, quant

        def turn(tile_qc, t_group):
            bank = psum.tile([P, HID], F32, tag="bank")
            for q in range(GROUPS):
                first = q * CHUNK + t_group * P
                nc.tensor.transpose(bank[:, q * P : (q + 1) * P], tile_qc[:, first : first + P], ident[:])
            return bank

        def out_job(c, t_group):
            state = {}

            def bring():
                bank = turn(product[c], t_group)
                numerator = pool.tile([P, HID], F32, tag="numerator", bufs=4)
                nc.vector.scalar_tensor_tensor(
                    out=numerator[:],
                    in0=bank[:],
                    scalar=0.5,
                    in1=h_rows[c][:, t_group * HID : (t_group + 1) * HID],
                    op0=ALU.mult,
                    op1=ALU.subtract,
                )
                state[0] = turn(denom[c], t_group), numerator

            def finish():
                bank, numerator = state[0]
                rows_out = pool.tile([P, HID], F32, tag="rows_out", bufs=6)
                nc.vector.tensor_tensor(out=rows_out[:], in0=bank[:], in1=numerator[:], op=ALU.mult)
                nc.sync.dma_start(out=out_dram[c][:, t_group, :], in_=rows_out[:])

            return bring, finish

        def run(jobs):
            waiting = None
            for first, second in jobs:
                first()
                if waiting is not None:
                    waiting()
                waiting = second
            if waiting is not None:
                waiting()

        def time_constant(c, u):
            h_bf16 = h_words[c][:].bitcast(BF16).rearrange("p (u c e) -> p u e c", u=PAIR, e=PAIR)
            for q in (2 * u, 2 * u + 1):
                z = psum.tile([P, CHUNK], F32, tag="bank")
                for k_group in range(PACK):
                    nc.tensor.matmul(
                        out=z[:],
                        lhsT=wt_cells[:, k_group, q * P : (q + 1) * P],
                        rhs=h_bf16[:, k_group // PAIR, k_group % PAIR, :],
                        start=(k_group == 0),
                        stop=(k_group == PACK - 1),
                    )
                nc.scalar.activation(
                    out=denom[c][:, q * CHUNK : (q + 1) * CHUNK],
                    in_=z[:],
                    func=ACT.Exp,
                    bias=vector_column(ROW_B_TAU, q),
                    scale=1.0,
                )

        def logarithms(chunks):
            for c in chunks:
                nc.scalar.activation(out=denom[c][:], in_=denom[c][:], func=ACT.Ln, bias=ones[:], scale=1.0)
            for c in chunks:
                for q in range(GROUPS):
                    cols = slice(q * CHUNK, (q + 1) * CHUNK)
                    nc.scalar.activation(
                        out=denom[c][:, cols],
                        in_=denom[c][:, cols],
                        func=ACT.Abs_reciprocal_sqrt,
                        bias=leak[:, q : q + 1],
                        scale=1.0,
                    )

        def reciprocal(c, u):
            pair = group_pair(denom[c], u)
            (nc.vector if RSQ == "V" else nc.gpsimd).tensor_tensor(out=pair, in0=pair, in1=pair, op=ALU.mult)

        def group_pair(tile_ap, u):
            return tile_ap[:, u * PAIR * CHUNK : (u + 1) * PAIR * CHUNK]

        def gate_times_dynamics(c, u, by_half=True):
            dynamics = pool.tile([P, PAIR * CHUNK], F32, tag="dynamics", bufs=3)
            targets = {GATE: group_pair(product[c], u), DYNAMICS: dynamics[:]}
            order = [(half, e) for half in (GATE, DYNAMICS) for e in range(PAIR)]
            if not by_half:
                order = [(half, e) for e in range(PAIR) for half in (GATE, DYNAMICS)]
            for half, e in order:
                    q = 2 * u + e
                    acc = psum.tile([P, CHUNK], F32, tag="bank")
                    for k_pass in (PASS_H, PASS_XC):
                        first = (2 * k_pass + half) * HID + q * P
                        nc.tensor.matmul_mx(
                            out=acc[:],
                            lhsT=w_codes[:, first : first + P].bitcast(FP8X4),
                            lhsT_scale=w_scales[:, first : first + P],
                            rhs=codes[(c, k_pass)][:].bitcast(FP8X4),
                            rhs_scale=scales[(c, k_pass)][:],
                            start=(k_pass == PASS_H),
                            stop=(k_pass == PASS_XC),
                        )
                    nc.scalar.activation(
                        out=targets[half][:, e * CHUNK : (e + 1) * CHUNK],
                        in_=acc[:],
                        func=ACT.Tanh,
                        bias=half_b_gate[:, q : q + 1] if half == GATE else vector_column(ROW_B_DYN, q),
                        scale=0.5 if half == GATE else 1.0,
                    )
                    if not by_half and half == DYNAMICS:
                        cell = product[c][:, q * CHUNK : (q + 1) * CHUNK]
                        nc.vector.scalar_tensor_tensor(
                            out=cell, in0=cell, scalar=1.0, in1=dynamics[:, e * CHUNK : (e + 1) * CHUNK], op0=ALU.add, op1=ALU.mult
                        )
            return dynamics

        def multiply(c, u, dynamics):
            pair = group_pair(product[c], u)
            nc.vector.scalar_tensor_tensor(
                out=pair, in0=pair, scalar=1.0, in1=dynamics[:], op0=ALU.add, op1=ALU.mult
            )

        def chunks_of(r):
            return list(range(sum(ROUNDS[:r]), sum(ROUNDS[: r + 1]))) if 0 <= r < len(ROUNDS) else []

        leak_exp = const.tile([P, 2 * GROUPS], F32)
        leak_softplus = const.tile([P, 2 * GROUPS], F32)
        leak_sum = const.tile([P, GROUPS], F32)
        leak = const.tile([P, GROUPS], F32)
        wt_t = const.tile([P, PACK * HID], BF16)
        wt_cells = wt_t[:].rearrange("p (k c) -> p k c", k=PACK)
        wt_split = wt_t[:].rearrange("p (u e c) -> p u e c", u=PAIR, e=PAIR)
        wt_banks = transpose_rows(wt_in[:], True)
        for b in range(2):
            (nc.vector.tensor_copy if b else nc.scalar.copy)(
                out=wt_split[:, :, :, b * HALF : (b + 1) * HALF],
                in_=wt_banks[b][:].bitcast(BF16).rearrange("p (u c e) -> p u e c", u=PAIR, e=PAIR),
            )

        first_h = [h_job(c) for c in chunks_of(0)]
        first_h[0][0]()
        vectors = const.tile([P, N_VECTORS * GROUPS], F32)
        vec_bank = psum.tile([P, GROUPS * P], BF16, tag="bank")
        for q in range(GROUPS):
            nc.tensor.transpose(vec_bank[:, q * P : (q + 1) * P], vec_rows[:, q * P : (q + 1) * P], ident_bf16[:])
        nc.vector.tensor_copy(
            out=vectors[:].rearrange("p (r q) -> p r q", q=GROUPS),
            in_=vec_bank[:].rearrange("p (q r) -> p r q", q=GROUPS)[:, 0:N_VECTORS, :],
        )

        def vector_column(row, q):
            return vectors[:, row * GROUPS + q : row * GROUPS + q + 1]

        half_b_gate = const.tile([P, GROUPS], F32)
        nc.vector.tensor_scalar_mul(
            out=half_b_gate[:], in0=vectors[:, ROW_B_GATE * GROUPS : (ROW_B_GATE + 1) * GROUPS], scalar1=0.5
        )
        for n, (bring, quant) in enumerate(first_h):
            if n:
                bring()
            quant()

        for c in chunks_of(0):
            load_xc(c)
        for c in chunks_of(1):
            if c not in h_rows:
                load_h(c)

        def time_constants(chunks):
            for c in chunks:
                d = pool.tile([P, GROUPS * CHUNK], F32, tag="denom", bufs=DEN)
                denom[c] = d
                for u in range(PAIR):
                    time_constant(c, u)

        time_constants(chunks_of(0))
        nc.scalar.activation(out=leak_exp[:], in_=vectors[:, ROW_GLEAK * GROUPS :], func=ACT.Exp)
        nc.scalar.activation(out=leak_softplus[:], in_=leak_exp[:], func=ACT.Ln, bias=ones[:], scale=1.0)
        nc.gpsimd.tensor_tensor(
            out=leak_sum[:], in0=leak_softplus[:, 0:GROUPS], in1=leak_softplus[:, GROUPS:], op=ALU.add
        )
        nc.gpsimd.tensor_scalar(out=leak[:], in0=leak_sum[:], scalar1=1e-6, scalar2=1.0, op0=ALU.add, op1=ALU.mult)

        w_codes = const.tile([P, 2 * 2 * HID], U32, align_bytes=256)
        w_scales = const.tile([P, 2 * 2 * HID], U8, align_bytes=256)
        jobs = [w_job(half, k_pass) for k_pass in (PASS_H, PASS_XC) for half in (GATE, DYNAMICS)]
        jobs += [h_job(c) for c in chunks_of(1)] + [xc_job(c) for c in chunks_of(0)]
        run(jobs)

        pending, left = [], []

        def put_out(n):
            run([pending.pop(0) for _ in range(min(n, len(pending)))])

        for r in range(len(ROUNDS)):
            now, ahead = chunks_of(r), chunks_of(r + 1)
            logarithms(now)
            for c in chunks_of(r + 2):
                load_h(c)
            for c in ahead:
                load_xc(c)
            run([pending.pop(0) for i in range(len(pending))] + left)
            for c in now:
                for u in range(PAIR):
                    reciprocal(c, u)
            time_constants(ahead)
            h_jobs, xc_jobs = [h_job(c) for c in chunks_of(r + 2)], [xc_job(c) for c in ahead]
            n_left = min(LEFT, len(xc_jobs))
            xc_jobs, left = xc_jobs[: len(xc_jobs) - n_left], xc_jobs[len(xc_jobs) - n_left :]
            jobs = h_jobs + xc_jobs if H_FIRST else xc_jobs + h_jobs
            waiting = None
            slot = 0
            for c in now:
                prod = pool.tile([P, GROUPS * CHUNK], F32, tag="product", bufs=PROD)
                product[c] = prod
                for u in range(PAIR):
                    last = SPLIT and not ahead and c == now[-1] and u == 1
                    dynamics = gate_times_dynamics(c, u, by_half=not last)
                    if slot >= FIRST_SLOT and (slot - FIRST_SLOT) % GROUP_JOBS == 0:
                        for bring, quant in [jobs.pop(0) for i in range(min(GROUP_JOBS, len(jobs)))]:
                            bring()
                            if waiting is not None:
                                waiting()
                            waiting = quant
                    slot += 1
                    if not last:
                        multiply(c, u, dynamics)
                    if not ahead:
                        put_out(OUT_LAST)
                pending += [out_job(c, t_group) for t_group in range(GROUPS)]
            for bring, quant in jobs:
                bring()
                waiting()
                waiting = quant
            if waiting is not None:
                waiting()
        put_out(len(pending))
